import numpy as np
import ml_dtypes


def mxq(x, axis, fmt="e4m3"):
    dtype, down = {"e4m3": (ml_dtypes.float8_e4m3fn, 7), "e5m2": (ml_dtypes.float8_e5m2, 14)}[fmt]
    v = np.moveaxis(np.asarray(x, np.float32).astype(ml_dtypes.bfloat16).astype(np.float64), axis, -1)
    blocks = v.reshape(v.shape[:-1] + (-1, 32))
    amax = np.abs(blocks).max(-1, keepdims=True)
    byte = np.maximum(np.where(amax > 0, np.frexp(amax)[1] - 1 + 127, 0) - down, 1)
    scale = np.exp2(byte - 127.0)
    codes = (blocks / scale).astype(np.float32).astype(dtype).astype(np.float64)
    return np.moveaxis((codes * scale).reshape(v.shape), -1, axis)


WIDE = False


def mx_kscale(k):
    if not WIDE:
        return np.ones(k)
    levels = np.array([10, -10, 5, -5, 0])
    a = np.random.permutation(np.resize(levels, k // 512 * 4)).reshape(k // 512, 4)
    idx = np.arange(k)
    return np.exp2(a[idx // 512, idx % 128 // 32])


BF16 = ml_dtypes.bfloat16


def bf(x):
    return np.asarray(x, np.float32).astype(BF16)


def f64(x):
    return np.asarray(x).astype(np.float64)


E2M1 = np.array([0.0, 0.5, 1.0, 1.5, 2.0, 3.0, 4.0, 6.0, -0.0, -0.5, -1.0, -1.5, -2.0, -3.0, -4.0, -6.0])


def pack_weight(w, fmt):
    k, n = w.shape
    w = f64(bf(w)).reshape(k // 32, 32, n)
    amax = np.abs(w).max(1)
    if fmt == "e4m3":
        byte = np.frexp(amax)[1] - 1 + 127 - 7
    else:
        mant, ex = np.frexp(amax / 6.0)
        byte = np.where(mant > 0.5, ex, ex - 1) + 127
    byte = np.clip(np.where(amax > 0, byte, 1), 1, 254)
    scaled = (w * np.exp2(127.0 - byte)[:, None, :]).reshape(k, n).astype(np.float32)
    by_word = np.ascontiguousarray(scaled.reshape(k // 512, 128, 4, n).transpose(0, 1, 3, 2))
    if fmt == "e4m3":
        words = by_word.astype(ml_dtypes.float8_e4m3fn).view(np.uint8)
    else:
        c = by_word.astype(ml_dtypes.float4_e2m1fn).view(np.uint8) & 0xF
        words = c[..., 0::2] | (c[..., 1::2] << 4)
    return np.ascontiguousarray(words), np.ascontiguousarray(byte.astype(np.uint8).reshape(k // 512, 16, n))


def unpack_weight(words, scales, fmt):
    g, p, n, _ = words.shape
    if fmt == "e4m3":
        vals = np.ascontiguousarray(words).view(ml_dtypes.float8_e4m3fn).astype(np.float64)
    else:
        nib = np.empty((g, p, n, 4), np.uint8)
        nib[..., 0::2] = words & 0xF
        nib[..., 1::2] = words >> 4
        vals = E2M1[nib]
    vals = vals * np.repeat(np.exp2(scales.astype(np.float64) - 127.0), 8, axis=1)[..., None]
    return vals.transpose(0, 1, 3, 2).reshape(g * 512, n)


N, S, F, M0, M1, M2 = 128, 1824, 4096, 128, 64, 32
MULS_LS = ((M0, 0), (M1, 1), (M2, 2))
NI = sum(m for m, l in MULS_LS)
ED = sum(m * (2 * l + 1) for m, l in MULS_LS)
C = S + NI
EPS = 1e-5
FMT = "e4m3"


def silu(v):
    return v / (1.0 + np.exp(-v))


def _blocks(x):
    outs, off = [], 0
    for mul, l in MULS_LS:
        d = 2 * l + 1
        outs.append(x[:, off:off + mul * d].reshape(x.shape[0], mul, d))
        off += mul * d
    return outs


def setup_inputs():
    s = np.array(mx_kscale(C), dtype=np.float64)
    s[S:] = 1.0
    xs = np.random.standard_normal((N, S)) + 0.5 * np.random.standard_normal((N, 1))
    xe = np.random.standard_normal((N, ED))
    xe[:, :M0] += 0.5 * np.random.standard_normal((N, 1))
    ln_w = bf((1.0 + 0.1 * np.random.standard_normal(S)) * s[:S])
    ln_b = bf(0.2 * np.random.standard_normal(S) * s[:S])
    W1_words, W1_scales = pack_weight(np.random.standard_normal((C, F)) / np.sqrt(C) / s[:, None], FMT)
    b1 = bf(0.2 * np.random.standard_normal(F))
    W2_words, W2_scales = pack_weight(np.random.standard_normal((F, C)) * 1.5 / np.sqrt(F), FMT)
    b2 = bf(0.2 * np.random.standard_normal(C))
    return {"node_scalar": bf(xs),
            "node_equi": bf(xe),
            "ln_w": ln_w,
            "ln_b": ln_b,
            "W1_words": W1_words,
            "W1_scales": W1_scales,
            "b1": b1,
            "W2_words": W2_words,
            "W2_scales": W2_scales,
            "b2": b2}


def reference(node_scalar, node_equi, ln_w, ln_b, W1_words, W1_scales, b1, W2_words, W2_scales, b2):
    node_scalar, node_equi = f64(node_scalar), f64(node_equi)
    mu = node_scalar.mean(-1, keepdims=True)
    var = node_scalar.var(-1, keepdims=True)
    ns = (node_scalar - mu) / np.sqrt(var + EPS) * f64(ln_w) + f64(ln_b)
    eb = []
    for (mul, l), blk in zip(MULS_LS, _blocks(node_equi)):
        if l == 0:
            blk = blk - blk.mean(axis=1, keepdims=True)
        norm2 = (blk * blk).sum(-1, keepdims=True).mean(axis=1, keepdims=True)
        eb.append(blk / np.sqrt(norm2 + EPS))
    inv = np.concatenate([(blk * blk).sum(-1) / np.sqrt(2 * l + 1) for (mul, l), blk in zip(MULS_LS, eb)], axis=-1)
    cat = np.concatenate([ns, inv], axis=-1)
    a = (mxq(cat, 1, "e4m3") @ unpack_weight(W1_words, W1_scales, FMT)) + f64(b1)
    h = (mxq(silu(a), 1, "e4m3") @ unpack_weight(W2_words, W2_scales, FMT)) + f64(b2)
    d_scalar, gate = h[:, :S], h[:, S:]
    gparts = np.split(gate, [M0, M0 + M1], axis=-1)
    n = node_scalar.shape[0]
    d_equi = np.concatenate([(blk * g[:, :, None]).reshape(n, -1) for blk, g in zip(eb, gparts)], axis=-1)
    return np.concatenate([node_scalar + d_scalar, node_equi + d_equi], axis=-1)

@@ -1,0 +1,350 @@
+from contextlib import ExitStack
+
+import concourse.mybir as mybir
+from concourse.masks import make_identity
+
+F32 = mybir.dt.float32
+BF16 = mybir.dt.bfloat16
+I32 = mybir.dt.int32
+U32 = mybir.dt.uint32
+U8 = mybir.dt.uint8
+FP8X4 = mybir.dt.float8_e4m3fn_x4
+ALU = mybir.AluOpType
+ACT = mybir.ActivationFunctionType
+AXIS = mybir.AxisListType
+
+P = 128
+S = 1824
+ED = 480
+C = 2048
+F = 4096
+EPS = 1e-5
+BLOCKS = ((0, 0, 128, 1), (128, 128, 64, 3), (320, 192, 32, 5))
+
+K_GROUP = 512
+BANK = 512
+G1 = C // K_GROUP
+G2 = F // K_GROUP
+W1_HALF = F // 2
+W2_HALF = C // 2
+LN_CHUNK = S // 4
+
+ROW_LN_W = 0
+ROW_LN_B = 4
+ROW_B1 = 8
+ROW_B2 = 16
+
+FLOPS = 2 * P * C * F * 2
+
+
+def tile_interactionblock_w_kernel(
+    tc, node_scalar, node_equi, ln_w, ln_b, W1_words, W1_scales, b1, W2_words, W2_scales, b2, out
+):
+    nc = tc.nc
+    with ExitStack() as ctx:
+        ctx.enter_context(tc.manual_schedule())
+        keep = ctx.enter_context(tc.tile_pool(name="keep", bufs=1))
+        work = ctx.enter_context(tc.tile_pool(name="work", bufs=2))
+        psum = ctx.enter_context(tc.psum_pool(name="psum", bufs=8))
+
+        def new_bank():
+            bank = psum.tile([P, BANK], F32, tag="bank", name="bank")
+            return bank
+
+        vectors = keep.tile([P, BANK], BF16)
+        nc.vector.memset(vectors[:], 0.0)
+        w1_planes = keep.tile([P, F], U8, align_bytes=64)
+        w2_planes = keep.tile([P, G2 // 4, C], U8, align_bytes=64)
+        nc.vector.memset(w1_planes[:].bitcast(I32), 0)
+        nc.vector.memset(w2_planes[:].bitcast(I32), 0)
+
+        ident_bf16 = keep.tile([P, P], BF16)
+        make_identity(nc, ident_bf16[:])
+        ident_f32 = keep.tile([P, P], F32)
+        make_identity(nc, ident_f32[:])
+        minus_half = keep.tile([P, 3], F32)
+        nc.gpsimd.memset(minus_half[:], -0.5)
+
+        xs = keep.tile([P, S], BF16)
+        nc.sync.dma_start(out=xs[:], in_=node_scalar)
+        xe = keep.tile([P, ED], BF16)
+        nc.sync.dma_start(out=xe[:], in_=node_equi)
+
+        nc.scalar.dma_start(
+            out=vectors[ROW_B1 : ROW_B1 + 8, :], in_=b1.rearrange("(r c) -> r c", c=BANK)
+        )
+        nc.scalar.dma_start(
+            out=vectors[ROW_B2 : ROW_B2 + 4, :], in_=b2.rearrange("(r c) -> r c", c=BANK)
+        )
+        nc.scalar.dma_start(
+            out=vectors[ROW_LN_W : ROW_LN_W + 4, 0:LN_CHUNK],
+            in_=ln_w.rearrange("(r c) -> r c", c=LN_CHUNK),
+        )
+        nc.scalar.dma_start(
+            out=vectors[ROW_LN_B : ROW_LN_B + 4, 0:LN_CHUNK],
+            in_=ln_b.rearrange("(r c) -> r c", c=LN_CHUNK),
+        )
+
+        for quad in range(4):
+            nc.sync.dma_start(
+                out=w1_planes[32 * quad : 32 * quad + 16, :].bitcast(I32),
+                in_=W1_scales[:, 4 * quad : 4 * quad + 4, :].bitcast(I32),
+            )
+        for four in range(G2 // 4):
+            for quad in range(4):
+                nc.sync.dma_start(
+                    out=w2_planes[32 * quad : 32 * quad + 16, four, :].bitcast(I32),
+                    in_=W2_scales[4 * four : 4 * four + 4, 4 * quad : 4 * quad + 4, :].bitcast(I32),
+                )
+
+        w1 = {}
+        for half in range(2):
+            for g in range(G1):
+                codes = keep.tile([P, W1_HALF], U32, name="w1_%d_%d" % (half, g), align_bytes=64)
+                flat = W1_words[g].rearrange("p n t -> p (n t)")
+                nc.sync.dma_start(
+                    out=codes[:].bitcast(I32),
+                    in_=flat[:, 4 * W1_HALF * half : 4 * W1_HALF * (half + 1)].bitcast(I32),
+                )
+                w1[(half, g)] = codes
+        w2_order = (1, 0)
+        w2 = {}
+        for half in w2_order:
+            for g in range(G2):
+                codes = keep.tile([P, W2_HALF], U32, name="w2_%d_%d" % (half, g), align_bytes=64)
+                flat = W2_words[g].rearrange("p n t -> p (n t)")
+                nc.sync.dma_start(
+                    out=codes[:].bitcast(I32),
+                    in_=flat[:, 4 * W2_HALF * half : 4 * W2_HALF * (half + 1)].bitcast(I32),
+                )
+                w2[(half, g)] = codes
+
+        def spread_two(row):
+            bank = psum.tile([P, 2, BANK], BF16, tag="bank", name="spread")
+            for i in range(2):
+                nc.tensor.matmul(
+                    out=bank[:, i, :],
+                    lhsT=ident_bf16[:, row + i : row + i + 1].to_broadcast([P, P]),
+                    rhs=vectors[:],
+                    start=True,
+                    stop=True,
+                )
+            return bank
+
+        def quantise_two_groups(values, codes, planes):
+            words = values.bitcast(F32)
+            bank = new_bank()
+            for i in range(2):
+                for u in range(2):
+                    nc.tensor.transpose(
+                        bank[:, (2 * i + u) * P : (2 * i + u + 1) * P],
+                        words[:, 256 * i + u : 256 * (i + 1) : 2],
+                        ident_f32[:],
+                    )
+            grouped = work.tile([P, 2 * K_GROUP], BF16, align_bytes=64)
+            nc.scalar.copy(
+                out=grouped[:].bitcast(F32).rearrange("p (i m u) -> p i m u", i=2, u=2),
+                in_=bank[:].rearrange("p (i u m) -> p i m u", i=2, u=2),
+            )
+            nc.vector.quantize_mx(out=codes.bitcast(FP8X4), scales=planes, in_=grouped[:])
+
+        scratch = keep.tile([P, ED], F32)
+        minus_mean0 = keep.tile([P, 1], F32)
+        nc.scalar.activation(
+            out=scratch[:, 0:P], in_=xe[:, 0:P], func=ACT.Copy, scale=-1.0 / P, accum_out=minus_mean0[:]
+        )
+        centred0 = keep.tile([P, P], F32)
+        nc.scalar.activation(out=centred0[:], in_=xe[:, 0:P], func=ACT.Identity, bias=minus_mean0[:])
+        block_in = [centred0[:]] + [
+            xe[:, col : col + channels * comps] for col, ch, channels, comps in BLOCKS[1:]
+        ]
+        mean_sq = keep.tile([P, 3], F32)
+        for l, (col, ch, channels, comps) in enumerate(BLOCKS):
+            nc.scalar.activation(
+                out=scratch[:, col : col + channels * comps],
+                in_=block_in[l],
+                func=ACT.Square,
+                scale=channels**-0.5,
+                accum_out=mean_sq[:, l : l + 1],
+            )
+        mean_sq_eps = keep.tile([P, 3], F32)
+        nc.gpsimd.tensor_scalar_add(mean_sq_eps[:], mean_sq[:], EPS)
+        eq_rnorm = keep.tile([P, 3], F32)
+        nc.gpsimd.tensor_tensor(out=eq_rnorm[:], in0=mean_sq_eps[:], in1=minus_half[:], op=ALU.pow)
+
+        ln_stats = keep.tile([P, 4, 6], F32)
+        for c in range(4):
+            nc.vector.bn_stats(out=ln_stats[:, c, :], in_=xs[:, c * LN_CHUNK : (c + 1) * LN_CHUNK])
+        ln_mean_var = keep.tile([P, 2], F32)
+        nc.vector.bn_aggr(out=ln_mean_var[:], in_=ln_stats[:].rearrange("p c s -> p (c s)"))
+        ln_var_eps = keep.tile([P, 1], F32)
+        nc.gpsimd.tensor_scalar_add(ln_var_eps[:], ln_mean_var[:, 1:2], EPS)
+        ln_rstd = keep.tile([P, 1], F32)
+        nc.gpsimd.tensor_tensor(out=ln_rstd[:], in0=ln_var_eps[:], in1=minus_half[:, 0:1], op=ALU.pow)
+
+        cat = keep.tile([P, C], BF16)
+        for two in range(2):
+            gain = spread_two(ROW_LN_W + 2 * two)
+            shift = spread_two(ROW_LN_B + 2 * two)
+            for i in range(2):
+                first = (2 * two + i) * LN_CHUNK
+                scaled = work.tile([P, LN_CHUNK], F32)
+                nc.vector.scalar_tensor_tensor(
+                    out=scaled[:],
+                    in0=xs[:, first : first + LN_CHUNK],
+                    scalar=ln_mean_var[:, 0:1],
+                    in1=gain[:, i, 0:LN_CHUNK],
+                    op0=ALU.subtract,
+                    op1=ALU.mult,
+                )
+                nc.vector.scalar_tensor_tensor(
+                    out=cat[:, first : first + LN_CHUNK],
+                    in0=scaled[:],
+                    scalar=ln_rstd[:],
+                    in1=shift[:, i, 0:LN_CHUNK],
+                    op0=ALU.mult,
+                    op1=ALU.add,
+                )
+
+        b1_all = keep.tile([P, F], BF16)
+        for two in range(F // (2 * BANK)):
+            bank = spread_two(ROW_B1 + 2 * two)
+            nc.scalar.copy(
+                out=b1_all[:, 2 * BANK * two : 2 * BANK * (two + 1)],
+                in_=bank[:].rearrange("p i n -> p (i n)"),
+            )
+
+        eb = keep.tile([P, ED], F32)
+        inv = keep.tile([P, C - S], F32)
+        for l, (col, ch, channels, comps) in enumerate(BLOCKS):
+            cols = slice(col, col + channels * comps)
+            nc.scalar.activation(
+                out=eb[:, cols], in_=block_in[l], func=ACT.Copy, scale=eq_rnorm[:, l : l + 1]
+            )
+            nc.scalar.activation(
+                out=scratch[:, cols], in_=eb[:, cols], func=ACT.Square, scale=comps**-0.25
+            )
+        for col, ch, channels, comps in BLOCKS:
+            nc.vector.tensor_reduce(
+                out=inv[:, ch : ch + channels],
+                in_=scratch[:, col : col + channels * comps].rearrange("p (c d) -> p c d", d=comps),
+                axis=AXIS.X,
+                op=ALU.add,
+            )
+        nc.vector.tensor_copy(out=cat[:, S:C], in_=inv[:])
+
+        cat_codes = keep.tile([P, G1, P], U32, align_bytes=64)
+        cat_planes = keep.tile([P, G1, P], U8, align_bytes=64)
+        for pair in range(G1 // 2):
+            groups = slice(2 * pair, 2 * pair + 2)
+            quantise_two_groups(
+                cat[:, 2 * K_GROUP * pair : 2 * K_GROUP * (pair + 1)],
+                cat_codes[:, groups, :].rearrange("p g m -> p (g m)"),
+                cat_planes[:, groups, :].rearrange("p g m -> p (g m)"),
+            )
+
+        addend = keep.tile([P, C], F32)
+        for two in range(C // (2 * BANK)):
+            bank = spread_two(ROW_B2 + 2 * two)
+            for i in range(2):
+                first = (2 * two + i) * BANK
+                width = min(BANK, S - first)
+                nc.vector.tensor_tensor(
+                    out=addend[:, first : first + width],
+                    in0=bank[:, i, 0:width],
+                    in1=xs[:, first : first + width],
+                    op=ALU.add,
+                )
+                if width < BANK:
+                    nc.vector.tensor_copy(
+                        out=addend[:, first + width : first + BANK], in_=bank[:, i, width:BANK]
+                    )
+
+        def layer1(half, acc, groups):
+            for g in groups:
+                for n in range(W1_HALF // BANK):
+                    nc.tensor.matmul_mx(
+                        out=acc[n][:],
+                        lhsT=cat_codes[:, g, :].bitcast(FP8X4),
+                        lhsT_scale=cat_planes[:, g, :],
+                        rhs=w1[(half, g)][:, n * BANK : (n + 1) * BANK].bitcast(FP8X4),
+                        rhs_scale=w1_planes[
+                            4 * g : P, half * W1_HALF + n * BANK : half * W1_HALF + (n + 1) * BANK
+                        ],
+                        start=(g == 0),
+                        stop=(g == G1 - 1),
+                    )
+
+        h_codes = keep.tile([P, G2, P], U32, align_bytes=64)
+        h_planes = keep.tile([P, G2, P], U8, align_bytes=64)
+
+        def silu_two_groups(pair, banks):
+            h = work.tile([P, 2 * K_GROUP], BF16)
+            for i in range(2):
+                first = (2 * pair + i) * BANK
+                biased = work.tile([P, BANK], F32)
+                nc.vector.tensor_tensor(
+                    out=biased[:], in0=banks[i][:], in1=b1_all[:, first : first + BANK], op=ALU.add
+                )
+                nc.scalar.activation(out=h[:, i * BANK : (i + 1) * BANK], in_=biased[:], func=ACT.Silu)
+            return h
+
+        def activate(half, acc):
+            hs = [silu_two_groups(2 * half + j, acc[2 * j : 2 * j + 2]) for j in range(2)]
+            for j in range(2):
+                groups = slice(4 * half + 2 * j, 4 * half + 2 * j + 2)
+                quantise_two_groups(
+                    hs[j][:],
+                    h_codes[:, groups, :].rearrange("p g m -> p (g m)"),
+                    h_planes[:, groups, :].rearrange("p g m -> p (g m)"),
+                )
+
+        acc_a = [new_bank() for n in range(W1_HALF // BANK)]
+        layer1(0, acc_a, range(G1))
+        acc_b = [new_bank() for n in range(W1_HALF // BANK)]
+        layer1(1, acc_b, range(G1 - 1))
+        activate(0, acc_a)
+        layer1(1, acc_b, range(G1 - 1, G1))
+        activate(1, acc_b)
+
+        summed = keep.tile([P, C], F32)
+        new_equi = keep.tile([P, ED], F32)
+        for half in w2_order:
+            acc = [new_bank() for n in range(W2_HALF // BANK)]
+            for g in range(G2):
+                for n in range(W2_HALF // BANK):
+                    first = half * W2_HALF + n * BANK
+                    nc.tensor.matmul_mx(
+                        out=acc[n][:],
+                        lhsT=h_codes[:, g, :].bitcast(FP8X4),
+                        lhsT_scale=h_planes[:, g, :],
+                        rhs=w2[(half, g)][:, n * BANK : (n + 1) * BANK].bitcast(FP8X4),
+                        rhs_scale=w2_planes[4 * (g % 4) : P, g // 4, first : first + BANK],
+                        start=(g == 0),
+                        stop=(g == G2 - 1),
+                    )
+            for n in range(W2_HALF // BANK):
+                first = half * W2_HALF + n * BANK
+                nc.vector.tensor_tensor(
+                    out=summed[:, first : first + BANK],
+                    in0=acc[n][:],
+                    in1=addend[:, first : first + BANK],
+                    op=ALU.add,
+                )
+                width = min(BANK, S - first)
+                nc.sync.dma_start(
+                    out=out[:, first : first + width], in_=summed[:, first : first + width]
+                )
+            if half == 1:
+                for col, ch, channels, comps in BLOCKS:
+                    cols = slice(col, col + channels * comps)
+                    nc.vector.tensor_tensor(
+                        out=new_equi[:, cols].rearrange("p (c d) -> p c d", d=comps),
+                        in0=eb[:, cols].rearrange("p (c d) -> p c d", d=comps),
+                        in1=summed[:, S + ch : S + ch + channels]
+                        .unsqueeze(2)
+                        .to_broadcast([P, channels, comps]),
+                        op=ALU.mult,
+                    )
+                nc.vector.tensor_tensor(out=new_equi[:], in0=new_equi[:], in1=xe[:], op=ALU.add)
+                nc.sync.dma_start(out=out[:, S : S + ED], in_=new_equi[:])

@@ -85,17 +85,14 @@ def tile_interactionblock_w_kernel(
             in_=ln_b.rearrange("(r c) -> r c", c=LN_CHUNK),
         )
 
-        for quad in range(4):
-            nc.sync.dma_start(
-                out=w1_planes[32 * quad : 32 * quad + 16, :].bitcast(I32),
-                in_=W1_scales[:, 4 * quad : 4 * quad + 4, :].bitcast(I32),
-            )
-        for four in range(G2 // 4):
+        def load_planes(planes, scales):
             for quad in range(4):
-                nc.sync.dma_start(
-                    out=w2_planes[32 * quad : 32 * quad + 16, four, :].bitcast(I32),
-                    in_=W2_scales[4 * four : 4 * four + 4, 4 * quad : 4 * quad + 4, :].bitcast(I32),
+                nc.gpsimd.dma_start(
+                    out=planes[32 * quad : 32 * quad + 16, :].bitcast(F32),
+                    in_=scales[:, 4 * quad : 4 * quad + 4, :].bitcast(F32),
                 )
+
+        load_planes(w1_planes, W1_scales)
 
         w1 = {}
         for half in range(2):
@@ -181,6 +178,9 @@ def tile_interactionblock_w_kernel(
         nc.gpsimd.tensor_scalar_add(ln_var_eps[:], ln_mean_var[:, 1:2], EPS)
         ln_rstd = keep.tile([P, 1], F32)
         nc.gpsimd.tensor_tensor(out=ln_rstd[:], in0=ln_var_eps[:], in1=minus_half[:, 0:1], op=ALU.pow)
+
+        for four in range(G2 // 4):
+            load_planes(w2_planes[:, four, :], W2_scales[4 * four : 4 * four + 4])
 
         cat = keep.tile([P, C], BF16)
         for two in range(2):

@@ -110,10 +110,15 @@ def tile_interactionblock_w_kernel(
             for g in range(G2):
                 codes = keep.tile([P, W2_HALF], U32, name="w2_%d_%d" % (half, g), align_bytes=64)
                 flat = W2_words[g].rearrange("p n t -> p (n t)")
-                nc.sync.dma_start(
-                    out=codes[:].bitcast(I32),
-                    in_=flat[:, 4 * W2_HALF * half : 4 * W2_HALF * (half + 1)].bitcast(I32),
-                )
+                is_last = half == w2_order[-1] and g == G2 - 1
+                step = BANK if is_last else W2_HALF
+                for first in range(0, W2_HALF, step):
+                    nc.sync.dma_start(
+                        out=codes[:, first : first + step].bitcast(I32),
+                        in_=flat[
+                            :, 4 * (W2_HALF * half + first) : 4 * (W2_HALF * half + first + step)
+                        ].bitcast(I32),
+                    )
                 w2[(half, g)] = codes
 
         def spread_two(row):
@@ -214,6 +219,8 @@ def tile_interactionblock_w_kernel(
                 in_=bank[:].rearrange("p i n -> p (i n)"),
             )
 
+        b2_banks = [spread_two(ROW_B2 + 2 * two) for two in range(C // (2 * BANK))]
+
         eb = keep.tile([P, ED], F32)
         inv = keep.tile([P, C - S], F32)
         for l, (col, ch, channels, comps) in enumerate(BLOCKS):
@@ -245,7 +252,7 @@ def tile_interactionblock_w_kernel(
 
         addend = keep.tile([P, C], F32)
         for two in range(C // (2 * BANK)):
-            bank = spread_two(ROW_B2 + 2 * two)
+            bank = b2_banks[two]
             for i in range(2):
                 first = (2 * two + i) * BANK
                 width = min(BANK, S - first)
@@ -299,19 +306,8 @@ def tile_interactionblock_w_kernel(
                     h_planes[:, groups, :].rearrange("p g m -> p (g m)"),
                 )
 
-        acc_a = [new_bank() for n in range(W1_HALF // BANK)]
-        layer1(0, acc_a, range(G1))
-        acc_b = [new_bank() for n in range(W1_HALF // BANK)]
-        layer1(1, acc_b, range(G1 - 1))
-        activate(0, acc_a)
-        layer1(1, acc_b, range(G1 - 1, G1))
-        activate(1, acc_b)
-
-        summed = keep.tile([P, C], F32)
-        new_equi = keep.tile([P, ED], F32)
-        for half in w2_order:
-            acc = [new_bank() for n in range(W2_HALF // BANK)]
-            for g in range(G2):
+        def layer2(half, acc, groups):
+            for g in groups:
                 for n in range(W2_HALF // BANK):
                     first = half * W2_HALF + n * BANK
                     nc.tensor.matmul_mx(
@@ -323,6 +319,10 @@ def tile_interactionblock_w_kernel(
                         start=(g == 0),
                         stop=(g == G2 - 1),
                     )
+
+        summed = keep.tile([P, C], F32)
+
+        def finish(half, acc):
             for n in range(W2_HALF // BANK):
                 first = half * W2_HALF + n * BANK
                 nc.vector.tensor_tensor(
@@ -335,16 +335,31 @@ def tile_interactionblock_w_kernel(
                 nc.sync.dma_start(
                     out=out[:, first : first + width], in_=summed[:, first : first + width]
                 )
-            if half == 1:
-                for col, ch, channels, comps in BLOCKS:
-                    cols = slice(col, col + channels * comps)
-                    nc.vector.tensor_tensor(
-                        out=new_equi[:, cols].rearrange("p (c d) -> p c d", d=comps),
-                        in0=eb[:, cols].rearrange("p (c d) -> p c d", d=comps),
-                        in1=summed[:, S + ch : S + ch + channels]
-                        .unsqueeze(2)
-                        .to_broadcast([P, channels, comps]),
-                        op=ALU.mult,
-                    )
-                nc.vector.tensor_tensor(out=new_equi[:], in0=new_equi[:], in1=xe[:], op=ALU.add)
-                nc.sync.dma_start(out=out[:, S : S + ED], in_=new_equi[:])
+
+        acc_a = [new_bank() for n in range(W1_HALF // BANK)]
+        layer1(0, acc_a, range(G1))
+        acc_b = [new_bank() for n in range(W1_HALF // BANK)]
+        layer1(1, acc_b, range(G1 - 1))
+        activate(0, acc_a)
+        layer1(1, acc_b, range(G1 - 1, G1))
+        acc_upper = [new_bank() for n in range(W2_HALF // BANK)]
+        layer2(1, acc_upper, range(G2 // 2))
+        activate(1, acc_b)
+        layer2(1, acc_upper, range(G2 // 2, G2))
+        finish(1, acc_upper)
+
+        new_equi = keep.tile([P, ED], F32)
+        for col, ch, channels, comps in BLOCKS:
+            cols = slice(col, col + channels * comps)
+            nc.vector.tensor_tensor(
+                out=new_equi[:, cols].rearrange("p (c d) -> p c d", d=comps),
+                in0=eb[:, cols].rearrange("p (c d) -> p c d", d=comps),
+                in1=summed[:, S + ch : S + ch + channels].unsqueeze(2).to_broadcast([P, channels, comps]),
+                op=ALU.mult,
+            )
+        nc.vector.tensor_tensor(out=new_equi[:], in0=new_equi[:], in1=xe[:], op=ALU.add)
+        nc.sync.dma_start(out=out[:, S : S + ED], in_=new_equi[:])
+
+        acc_lower = [new_bank() for n in range(W2_HALF // BANK)]
+        layer2(0, acc_lower, range(G2))
+        finish(0, acc_lower)

@@ -52,11 +52,10 @@ def tile_interactionblock_w_kernel(
             return bank
 
         vectors = keep.tile([P, BANK], BF16)
-        nc.vector.memset(vectors[:], 0.0)
+        nc.vector.memset(vectors[:].bitcast(I32), 0)
         w1_planes = keep.tile([P, F], U8, align_bytes=64)
         w2_planes = keep.tile([P, G2 // 4, C], U8, align_bytes=64)
         nc.vector.memset(w1_planes[:].bitcast(I32), 0)
-        nc.vector.memset(w2_planes[:].bitcast(I32), 0)
 
         ident_bf16 = keep.tile([P, P], BF16)
         make_identity(nc, ident_bf16[:])
@@ -71,18 +70,18 @@ def tile_interactionblock_w_kernel(
         nc.sync.dma_start(out=xe[:], in_=node_equi)
 
         nc.scalar.dma_start(
-            out=vectors[ROW_B1 : ROW_B1 + 8, :], in_=b1.rearrange("(r c) -> r c", c=BANK)
-        )
-        nc.scalar.dma_start(
-            out=vectors[ROW_B2 : ROW_B2 + 4, :], in_=b2.rearrange("(r c) -> r c", c=BANK)
-        )
-        nc.scalar.dma_start(
             out=vectors[ROW_LN_W : ROW_LN_W + 4, 0:LN_CHUNK],
             in_=ln_w.rearrange("(r c) -> r c", c=LN_CHUNK),
         )
         nc.scalar.dma_start(
             out=vectors[ROW_LN_B : ROW_LN_B + 4, 0:LN_CHUNK],
             in_=ln_b.rearrange("(r c) -> r c", c=LN_CHUNK),
+        )
+        nc.scalar.dma_start(
+            out=vectors[ROW_B1 : ROW_B1 + 8, :], in_=b1.rearrange("(r c) -> r c", c=BANK)
+        )
+        nc.scalar.dma_start(
+            out=vectors[ROW_B2 : ROW_B2 + 4, :], in_=b2.rearrange("(r c) -> r c", c=BANK)
         )
 
         def load_planes(planes, scales):
@@ -133,7 +132,7 @@ def tile_interactionblock_w_kernel(
                 )
             return bank
 
-        def quantise_two_groups(values, codes, planes):
+        def transpose_two_groups(values):
             words = values.bitcast(F32)
             bank = new_bank()
             for i in range(2):
@@ -148,7 +147,7 @@ def tile_interactionblock_w_kernel(
                 out=grouped[:].bitcast(F32).rearrange("p (i m u) -> p i m u", i=2, u=2),
                 in_=bank[:].rearrange("p (i u m) -> p i m u", i=2, u=2),
             )
-            nc.vector.quantize_mx(out=codes.bitcast(FP8X4), scales=planes, in_=grouped[:])
+            return grouped
 
         scratch = keep.tile([P, ED], F32)
         minus_mean0 = keep.tile([P, 1], F32)
@@ -184,42 +183,11 @@ def tile_interactionblock_w_kernel(
         ln_rstd = keep.tile([P, 1], F32)
         nc.gpsimd.tensor_tensor(out=ln_rstd[:], in0=ln_var_eps[:], in1=minus_half[:, 0:1], op=ALU.pow)
 
-        for four in range(G2 // 4):
-            load_planes(w2_planes[:, four, :], W2_scales[4 * four : 4 * four + 4])
-
-        cat = keep.tile([P, C], BF16)
+        gains, shifts = [], []
         for two in range(2):
-            gain = spread_two(ROW_LN_W + 2 * two)
-            shift = spread_two(ROW_LN_B + 2 * two)
-            for i in range(2):
-                first = (2 * two + i) * LN_CHUNK
-                scaled = work.tile([P, LN_CHUNK], F32)
-                nc.vector.scalar_tensor_tensor(
-                    out=scaled[:],
-                    in0=xs[:, first : first + LN_CHUNK],
-                    scalar=ln_mean_var[:, 0:1],
-                    in1=gain[:, i, 0:LN_CHUNK],
-                    op0=ALU.subtract,
-                    op1=ALU.mult,
-                )
-                nc.vector.scalar_tensor_tensor(
-                    out=cat[:, first : first + LN_CHUNK],
-                    in0=scaled[:],
-                    scalar=ln_rstd[:],
-                    in1=shift[:, i, 0:LN_CHUNK],
-                    op0=ALU.mult,
-                    op1=ALU.add,
-                )
-
-        b1_all = keep.tile([P, F], BF16)
-        for two in range(F // (2 * BANK)):
-            bank = spread_two(ROW_B1 + 2 * two)
-            nc.scalar.copy(
-                out=b1_all[:, 2 * BANK * two : 2 * BANK * (two + 1)],
-                in_=bank[:].rearrange("p i n -> p (i n)"),
-            )
-
-        b2_banks = [spread_two(ROW_B2 + 2 * two) for two in range(C // (2 * BANK))]
+            gains.append(spread_two(ROW_LN_W + 2 * two))
+            shifts.append(spread_two(ROW_LN_B + 2 * two))
+        b1_banks = [spread_two(ROW_B1 + 2 * two) for two in range(F // (2 * BANK))]
 
         eb = keep.tile([P, ED], F32)
         inv = keep.tile([P, C - S], F32)
@@ -231,6 +199,57 @@ def tile_interactionblock_w_kernel(
             nc.scalar.activation(
                 out=scratch[:, cols], in_=eb[:, cols], func=ACT.Square, scale=comps**-0.25
             )
+
+        b1_all = keep.tile([P, F], BF16)
+
+        def keep_b1(two):
+            nc.scalar.copy(
+                out=b1_all[:, 2 * BANK * two : 2 * BANK * (two + 1)],
+                in_=b1_banks[two][:].rearrange("p i n -> p (i n)"),
+            )
+
+        cat = keep.tile([P, C], BF16)
+
+        def norm_quarter(c):
+            first = c * LN_CHUNK
+            scaled = work.tile([P, LN_CHUNK], F32)
+            nc.vector.scalar_tensor_tensor(
+                out=scaled[:],
+                in0=xs[:, first : first + LN_CHUNK],
+                scalar=ln_mean_var[:, 0:1],
+                in1=gains[c // 2][:, c % 2, 0:LN_CHUNK],
+                op0=ALU.subtract,
+                op1=ALU.mult,
+            )
+            nc.vector.scalar_tensor_tensor(
+                out=cat[:, first : first + LN_CHUNK],
+                in0=scaled[:],
+                scalar=ln_rstd[:],
+                in1=shifts[c // 2][:, c % 2, 0:LN_CHUNK],
+                op0=ALU.mult,
+                op1=ALU.add,
+            )
+
+        cat_codes = keep.tile([P, G1, P], U32, align_bytes=64)
+        cat_planes = keep.tile([P, G1, P], U8, align_bytes=64)
+
+        def transpose_cat(pair):
+            return transpose_two_groups(cat[:, 2 * K_GROUP * pair : 2 * K_GROUP * (pair + 1)])
+
+        def quantise_cat(pair, grouped):
+            groups = slice(2 * pair, 2 * pair + 2)
+            nc.vector.quantize_mx(
+                out=cat_codes[:, groups, :].rearrange("p g m -> p (g m)").bitcast(FP8X4),
+                scales=cat_planes[:, groups, :].rearrange("p g m -> p (g m)"),
+                in_=grouped[:],
+            )
+
+        norm_quarter(0)
+        norm_quarter(1)
+        norm_quarter(2)
+        keep_b1(0)
+        keep_b1(1)
+        grouped0 = transpose_cat(0)
         for col, ch, channels, comps in BLOCKS:
             nc.vector.tensor_reduce(
                 out=inv[:, ch : ch + channels],
@@ -239,16 +258,17 @@ def tile_interactionblock_w_kernel(
                 op=ALU.add,
             )
         nc.vector.tensor_copy(out=cat[:, S:C], in_=inv[:])
+        norm_quarter(3)
+        quantise_cat(0, grouped0)
+        grouped1 = transpose_cat(1)
+        keep_b1(2)
+        keep_b1(3)
+        b2_banks = [spread_two(ROW_B2 + 2 * two) for two in range(C // (2 * BANK))]
 
-        cat_codes = keep.tile([P, G1, P], U32, align_bytes=64)
-        cat_planes = keep.tile([P, G1, P], U8, align_bytes=64)
-        for pair in range(G1 // 2):
-            groups = slice(2 * pair, 2 * pair + 2)
-            quantise_two_groups(
-                cat[:, 2 * K_GROUP * pair : 2 * K_GROUP * (pair + 1)],
-                cat_codes[:, groups, :].rearrange("p g m -> p (g m)"),
-                cat_planes[:, groups, :].rearrange("p g m -> p (g m)"),
-            )
+        nc.vector.memset(w2_planes[:].bitcast(I32), 0)
+        quantise_cat(1, grouped1)
+        for four in range(G2 // 4):
+            load_planes(w2_planes[:, four, :], W2_scales[4 * four : 4 * four + 4])
 
         addend = keep.tile([P, C], F32)
         for two in range(C // (2 * BANK)):
@@ -300,10 +320,11 @@ def tile_interactionblock_w_kernel(
             hs = [silu_two_groups(2 * half + j, acc[2 * j : 2 * j + 2]) for j in range(2)]
             for j in range(2):
                 groups = slice(4 * half + 2 * j, 4 * half + 2 * j + 2)
-                quantise_two_groups(
-                    hs[j][:],
-                    h_codes[:, groups, :].rearrange("p g m -> p (g m)"),
-                    h_planes[:, groups, :].rearrange("p g m -> p (g m)"),
+                grouped = transpose_two_groups(hs[j][:])
+                nc.vector.quantize_mx(
+                    out=h_codes[:, groups, :].rearrange("p g m -> p (g m)").bitcast(FP8X4),
+                    scales=h_planes[:, groups, :].rearrange("p g m -> p (g m)"),
+                    in_=grouped[:],
                 )
 
         def layer2(half, acc, groups):

@@ -31,8 +31,8 @@ LN_CHUNK = S // 4
 
 ROW_LN_W = 0
 ROW_LN_B = 4
-ROW_B1 = 8
-ROW_B2 = 16
+ROW_B1 = 0
+ROW_B2 = 8
 
 FLOPS = 2 * P * C * F * 2
 
@@ -51,37 +51,40 @@ def tile_interactionblock_w_kernel(
             bank = psum.tile([P, BANK], F32, tag="bank", name="bank")
             return bank
 
-        vectors = keep.tile([P, BANK], BF16)
-        nc.vector.memset(vectors[:].bitcast(I32), 0)
+        ln_rows = keep.tile([P, BANK], BF16)
+        nc.vector.memset(ln_rows[:].bitcast(I32), 0)
+        bias_rows = keep.tile([P, BANK], BF16)
+        nc.vector.memset(bias_rows[:].bitcast(I32), 0)
         w1_planes = keep.tile([P, F], U8, align_bytes=64)
         w2_planes = keep.tile([P, G2 // 4, C], U8, align_bytes=64)
         nc.vector.memset(w1_planes[:].bitcast(I32), 0)
+        nc.vector.memset(w2_planes[:].bitcast(I32), 0)
 
         ident_bf16 = keep.tile([P, P], BF16)
         make_identity(nc, ident_bf16[:])
         ident_f32 = keep.tile([P, P], F32)
         make_identity(nc, ident_f32[:])
-        minus_half = keep.tile([P, 3], F32)
+        minus_half = keep.tile([P, 4], F32)
         nc.gpsimd.memset(minus_half[:], -0.5)
 
         xs = keep.tile([P, S], BF16)
         nc.sync.dma_start(out=xs[:], in_=node_scalar)
+        nc.sync.dma_start(
+            out=ln_rows[ROW_LN_W : ROW_LN_W + 4, 0:LN_CHUNK],
+            in_=ln_w.rearrange("(r c) -> r c", c=LN_CHUNK),
+        )
+        nc.sync.dma_start(
+            out=ln_rows[ROW_LN_B : ROW_LN_B + 4, 0:LN_CHUNK],
+            in_=ln_b.rearrange("(r c) -> r c", c=LN_CHUNK),
+        )
         xe = keep.tile([P, ED], BF16)
         nc.sync.dma_start(out=xe[:], in_=node_equi)
 
         nc.scalar.dma_start(
-            out=vectors[ROW_LN_W : ROW_LN_W + 4, 0:LN_CHUNK],
-            in_=ln_w.rearrange("(r c) -> r c", c=LN_CHUNK),
+            out=bias_rows[ROW_B1 : ROW_B1 + 8, :], in_=b1.rearrange("(r c) -> r c", c=BANK)
         )
         nc.scalar.dma_start(
-            out=vectors[ROW_LN_B : ROW_LN_B + 4, 0:LN_CHUNK],
-            in_=ln_b.rearrange("(r c) -> r c", c=LN_CHUNK),
-        )
-        nc.scalar.dma_start(
-            out=vectors[ROW_B1 : ROW_B1 + 8, :], in_=b1.rearrange("(r c) -> r c", c=BANK)
-        )
-        nc.scalar.dma_start(
-            out=vectors[ROW_B2 : ROW_B2 + 4, :], in_=b2.rearrange("(r c) -> r c", c=BANK)
+            out=bias_rows[ROW_B2 : ROW_B2 + 4, :], in_=b2.rearrange("(r c) -> r c", c=BANK)
         )
 
         def load_planes(planes, scales):
@@ -120,7 +123,7 @@ def tile_interactionblock_w_kernel(
                     )
                 w2[(half, g)] = codes
 
-        def spread_two(row):
+        def spread_two(vectors, row):
             bank = psum.tile([P, 2, BANK], BF16, tag="bank", name="spread")
             for i in range(2):
                 nc.tensor.matmul(
@@ -159,42 +162,43 @@ def tile_interactionblock_w_kernel(
         block_in = [centred0[:]] + [
             xe[:, col : col + channels * comps] for col, ch, channels, comps in BLOCKS[1:]
         ]
-        mean_sq = keep.tile([P, 3], F32)
+        moments = keep.tile([P, 5], F32)
         for l, (col, ch, channels, comps) in enumerate(BLOCKS):
             nc.scalar.activation(
                 out=scratch[:, col : col + channels * comps],
                 in_=block_in[l],
                 func=ACT.Square,
                 scale=channels**-0.5,
-                accum_out=mean_sq[:, l : l + 1],
+                accum_out=moments[:, 2 + l : 3 + l],
             )
-        mean_sq_eps = keep.tile([P, 3], F32)
-        nc.gpsimd.tensor_scalar_add(mean_sq_eps[:], mean_sq[:], EPS)
-        eq_rnorm = keep.tile([P, 3], F32)
-        nc.gpsimd.tensor_tensor(out=eq_rnorm[:], in0=mean_sq_eps[:], in1=minus_half[:], op=ALU.pow)
 
         ln_stats = keep.tile([P, 4, 6], F32)
         for c in range(4):
             nc.vector.bn_stats(out=ln_stats[:, c, :], in_=xs[:, c * LN_CHUNK : (c + 1) * LN_CHUNK])
-        ln_mean_var = keep.tile([P, 2], F32)
-        nc.vector.bn_aggr(out=ln_mean_var[:], in_=ln_stats[:].rearrange("p c s -> p (c s)"))
-        ln_var_eps = keep.tile([P, 1], F32)
-        nc.gpsimd.tensor_scalar_add(ln_var_eps[:], ln_mean_var[:, 1:2], EPS)
-        ln_rstd = keep.tile([P, 1], F32)
-        nc.gpsimd.tensor_tensor(out=ln_rstd[:], in0=ln_var_eps[:], in1=minus_half[:, 0:1], op=ALU.pow)
+        nc.vector.bn_aggr(out=moments[:, 0:2], in_=ln_stats[:].rearrange("p c s -> p (c s)"))
+        ln_mean = moments[:, 0:1]
+
+        moments_eps = keep.tile([P, 4], F32)
+        nc.gpsimd.tensor_scalar_add(moments_eps[:], moments[:, 1:5], EPS)
+        rnorms = keep.tile([P, 4], F32)
+        nc.gpsimd.tensor_tensor(out=rnorms[:], in0=moments_eps[:], in1=minus_half[:], op=ALU.pow)
+        ln_rstd = rnorms[:, 0:1]
+
+        for four in range(G2 // 4):
+            load_planes(w2_planes[:, four, :], W2_scales[4 * four : 4 * four + 4])
 
         gains, shifts = [], []
         for two in range(2):
-            gains.append(spread_two(ROW_LN_W + 2 * two))
-            shifts.append(spread_two(ROW_LN_B + 2 * two))
-        b1_banks = [spread_two(ROW_B1 + 2 * two) for two in range(F // (2 * BANK))]
+            gains.append(spread_two(ln_rows, ROW_LN_W + 2 * two))
+            shifts.append(spread_two(ln_rows, ROW_LN_B + 2 * two))
+        b1_banks = [spread_two(bias_rows, ROW_B1 + 2 * two) for two in range(F // (2 * BANK))]
 
         eb = keep.tile([P, ED], F32)
         inv = keep.tile([P, C - S], F32)
         for l, (col, ch, channels, comps) in enumerate(BLOCKS):
             cols = slice(col, col + channels * comps)
             nc.scalar.activation(
-                out=eb[:, cols], in_=block_in[l], func=ACT.Copy, scale=eq_rnorm[:, l : l + 1]
+                out=eb[:, cols], in_=block_in[l], func=ACT.Copy, scale=rnorms[:, 1 + l : 2 + l]
             )
             nc.scalar.activation(
                 out=scratch[:, cols], in_=eb[:, cols], func=ACT.Square, scale=comps**-0.25
@@ -216,7 +220,7 @@ def tile_interactionblock_w_kernel(
             nc.vector.scalar_tensor_tensor(
                 out=scaled[:],
                 in0=xs[:, first : first + LN_CHUNK],
-                scalar=ln_mean_var[:, 0:1],
+                scalar=ln_mean,
                 in1=gains[c // 2][:, c % 2, 0:LN_CHUNK],
                 op0=ALU.subtract,
                 op1=ALU.mult,
@@ -224,7 +228,7 @@ def tile_interactionblock_w_kernel(
             nc.vector.scalar_tensor_tensor(
                 out=cat[:, first : first + LN_CHUNK],
                 in0=scaled[:],
-                scalar=ln_rstd[:],
+                scalar=ln_rstd,
                 in1=shifts[c // 2][:, c % 2, 0:LN_CHUNK],
                 op0=ALU.mult,
                 op1=ALU.add,
@@ -263,12 +267,9 @@ def tile_interactionblock_w_kernel(
         grouped1 = transpose_cat(1)
         keep_b1(2)
         keep_b1(3)
-        b2_banks = [spread_two(ROW_B2 + 2 * two) for two in range(C // (2 * BANK))]
+        b2_banks = [spread_two(bias_rows, ROW_B2 + 2 * two) for two in range(C // (2 * BANK))]
 
-        nc.vector.memset(w2_planes[:].bitcast(I32), 0)
         quantise_cat(1, grouped1)
-        for four in range(G2 // 4):
-            load_planes(w2_planes[:, four, :], W2_scales[4 * four : 4 * four + 4])
 
         addend = keep.tile([P, C], F32)
         for two in range(C // (2 * BANK)):

@@ -27,6 +27,7 @@ G1 = C // K_GROUP
 G2 = F // K_GROUP
 W1_HALF = F // 2
 W2_HALF = C // 2
+W2_PIECES = {1: (512, 512), 0: (512, 256, 128, 128)}
 LN_CHUNK = S // 4
 
 ROW_LN_W = 0
@@ -113,14 +114,15 @@ def tile_interactionblock_w_kernel(
                 codes = keep.tile([P, W2_HALF], U32, name="w2_%d_%d" % (half, g), align_bytes=64)
                 flat = W2_words[g].rearrange("p n t -> p (n t)")
                 is_last = half == w2_order[-1] and g == G2 - 1
-                step = BANK if is_last else W2_HALF
-                for first in range(0, W2_HALF, step):
+                first = 0
+                for width in W2_PIECES[half] if is_last else (W2_HALF,):
                     nc.sync.dma_start(
-                        out=codes[:, first : first + step].bitcast(I32),
+                        out=codes[:, first : first + width].bitcast(I32),
                         in_=flat[
-                            :, 4 * (W2_HALF * half + first) : 4 * (W2_HALF * half + first + step)
+                            :, 4 * (W2_HALF * half + first) : 4 * (W2_HALF * half + first + width)
                         ].bitcast(I32),
                     )
+                    first += width
                 w2[(half, g)] = codes
 
         def spread_two(vectors, row):
@@ -330,33 +332,34 @@ def tile_interactionblock_w_kernel(
 
         def layer2(half, acc, groups):
             for g in groups:
-                for n in range(W2_HALF // BANK):
-                    first = half * W2_HALF + n * BANK
+                first = 0
+                for n, width in enumerate(W2_PIECES[half]):
+                    cols = slice(half * W2_HALF + first, half * W2_HALF + first + width)
                     nc.tensor.matmul_mx(
-                        out=acc[n][:],
+                        out=acc[n][:, 0:width],
                         lhsT=h_codes[:, g, :].bitcast(FP8X4),
                         lhsT_scale=h_planes[:, g, :],
-                        rhs=w2[(half, g)][:, n * BANK : (n + 1) * BANK].bitcast(FP8X4),
-                        rhs_scale=w2_planes[4 * (g % 4) : P, g // 4, first : first + BANK],
+                        rhs=w2[(half, g)][:, first : first + width].bitcast(FP8X4),
+                        rhs_scale=w2_planes[4 * (g % 4) : P, g // 4, cols],
                         start=(g == 0),
                         stop=(g == G2 - 1),
                     )
+                    first += width
 
         summed = keep.tile([P, C], F32)
 
         def finish(half, acc):
-            for n in range(W2_HALF // BANK):
-                first = half * W2_HALF + n * BANK
+            first = half * W2_HALF
+            for n, width in enumerate(W2_PIECES[half]):
                 nc.vector.tensor_tensor(
-                    out=summed[:, first : first + BANK],
-                    in0=acc[n][:],
-                    in1=addend[:, first : first + BANK],
+                    out=summed[:, first : first + width],
+                    in0=acc[n][:, 0:width],
+                    in1=addend[:, first : first + width],
                     op=ALU.add,
                 )
-                width = min(BANK, S - first)
-                nc.sync.dma_start(
-                    out=out[:, first : first + width], in_=summed[:, first : first + width]
-                )
+                last = min(first + width, S)
+                nc.sync.dma_start(out=out[:, first:last], in_=summed[:, first:last])
+                first += width
 
         acc_a = [new_bank() for n in range(W1_HALF // BANK)]
         layer1(0, acc_a, range(G1))
@@ -364,7 +367,7 @@ def tile_interactionblock_w_kernel(
         layer1(1, acc_b, range(G1 - 1))
         activate(0, acc_a)
         layer1(1, acc_b, range(G1 - 1, G1))
-        acc_upper = [new_bank() for n in range(W2_HALF // BANK)]
+        acc_upper = [new_bank() for width in W2_PIECES[1]]
         layer2(1, acc_upper, range(G2 // 2))
         activate(1, acc_b)
         layer2(1, acc_upper, range(G2 // 2, G2))
@@ -382,6 +385,6 @@ def tile_interactionblock_w_kernel(
         nc.vector.tensor_tensor(out=new_equi[:], in0=new_equi[:], in1=xe[:], op=ALU.add)
         nc.sync.dma_start(out=out[:, S : S + ED], in_=new_equi[:])
 
-        acc_lower = [new_bank() for n in range(W2_HALF // BANK)]
+        acc_lower = [new_bank() for width in W2_PIECES[0]]
         layer2(0, acc_lower, range(G2))
         finish(0, acc_lower)

@@ -55,10 +55,10 @@ def tile_interactionblock_w_kernel(
         ln_rows = keep.tile([P, BANK], BF16)
         nc.vector.memset(ln_rows[:].bitcast(I32), 0)
         bias_rows = keep.tile([P, BANK], BF16)
-        nc.vector.memset(bias_rows[:].bitcast(I32), 0)
         w1_planes = keep.tile([P, F], U8, align_bytes=64)
         w2_planes = keep.tile([P, G2 // 4, C], U8, align_bytes=64)
         nc.vector.memset(w1_planes[:].bitcast(I32), 0)
+        nc.vector.memset(bias_rows[:].bitcast(I32), 0)
         nc.vector.memset(w2_planes[:].bitcast(I32), 0)
 
         ident_bf16 = keep.tile([P, P], BF16)
@@ -68,45 +68,44 @@ def tile_interactionblock_w_kernel(
         minus_half = keep.tile([P, 4], F32)
         nc.gpsimd.memset(minus_half[:], -0.5)
 
-        xs = keep.tile([P, S], BF16)
-        nc.sync.dma_start(out=xs[:], in_=node_scalar)
-        nc.sync.dma_start(
-            out=ln_rows[ROW_LN_W : ROW_LN_W + 4, 0:LN_CHUNK],
-            in_=ln_w.rearrange("(r c) -> r c", c=LN_CHUNK),
-        )
-        nc.sync.dma_start(
-            out=ln_rows[ROW_LN_B : ROW_LN_B + 4, 0:LN_CHUNK],
-            in_=ln_b.rearrange("(r c) -> r c", c=LN_CHUNK),
-        )
-        xe = keep.tile([P, ED], BF16)
-        nc.sync.dma_start(out=xe[:], in_=node_equi)
+        def load_rows(tile, row, vector, width):
+            rows = vector.rearrange("(r c) -> r c", c=width)
+            nc.sync.dma_start(out=tile[row : row + rows.shape[0], 0:width], in_=rows)
 
-        nc.scalar.dma_start(
-            out=bias_rows[ROW_B1 : ROW_B1 + 8, :], in_=b1.rearrange("(r c) -> r c", c=BANK)
-        )
-        nc.scalar.dma_start(
-            out=bias_rows[ROW_B2 : ROW_B2 + 4, :], in_=b2.rearrange("(r c) -> r c", c=BANK)
-        )
-
-        def load_planes(planes, scales):
-            for quad in range(4):
-                nc.gpsimd.dma_start(
-                    out=planes[32 * quad : 32 * quad + 16, :].bitcast(F32),
-                    in_=scales[:, 4 * quad : 4 * quad + 4, :].bitcast(F32),
+        def load_planes(engine, dtype, planes, scales, quads):
+            for quad in quads:
+                engine.dma_start(
+                    out=planes[32 * quad : 32 * quad + 16, :].bitcast(dtype),
+                    in_=scales[:, 4 * quad : 4 * quad + 4, :].bitcast(dtype),
                 )
-
-        load_planes(w1_planes, W1_scales)
 
         w1 = {}
-        for half in range(2):
-            for g in range(G1):
-                codes = keep.tile([P, W1_HALF], U32, name="w1_%d_%d" % (half, g), align_bytes=64)
-                flat = W1_words[g].rearrange("p n t -> p (n t)")
-                nc.sync.dma_start(
-                    out=codes[:].bitcast(I32),
-                    in_=flat[:, 4 * W1_HALF * half : 4 * W1_HALF * (half + 1)].bitcast(I32),
-                )
-                w1[(half, g)] = codes
+
+        def load_w1(half, g):
+            codes = keep.tile([P, W1_HALF], U32, name="w1_%d_%d" % (half, g), align_bytes=64)
+            flat = W1_words[g].rearrange("p n t -> p (n t)")
+            nc.sync.dma_start(
+                out=codes[:].bitcast(I32),
+                in_=flat[:, 4 * W1_HALF * half : 4 * W1_HALF * (half + 1)].bitcast(I32),
+            )
+            w1[(half, g)] = codes
+
+        xs = keep.tile([P, S], BF16)
+        nc.sync.dma_start(out=xs[:], in_=node_scalar)
+        xe = keep.tile([P, ED], BF16)
+        nc.sync.dma_start(out=xe[:], in_=node_equi)
+        load_rows(ln_rows, ROW_LN_W, ln_w, LN_CHUNK)
+        load_planes(nc.sync, I32, w1_planes, W1_scales, range(4))
+        load_w1(0, 0)
+        load_rows(ln_rows, ROW_LN_B, ln_b, LN_CHUNK)
+        load_w1(0, 1)
+        load_rows(bias_rows, ROW_B1, b1, BANK)
+        load_rows(bias_rows, ROW_B2, b2, BANK)
+        for half, g in ((0, 2), (0, 3), (1, 0), (1, 1), (1, 2), (1, 3)):
+            load_w1(half, g)
+
+        load_planes(nc.gpsimd, F32, w2_planes[:, 0, :], W2_scales[0:4], range(0, 2))
+
         w2_order = (1, 0)
         w2 = {}
         for half in w2_order:
@@ -186,8 +185,8 @@ def tile_interactionblock_w_kernel(
         nc.gpsimd.tensor_tensor(out=rnorms[:], in0=moments_eps[:], in1=minus_half[:], op=ALU.pow)
         ln_rstd = rnorms[:, 0:1]
 
-        for four in range(G2 // 4):
-            load_planes(w2_planes[:, four, :], W2_scales[4 * four : 4 * four + 4])
+        load_planes(nc.gpsimd, F32, w2_planes[:, 0, :], W2_scales[0:4], range(2, 4))
+        load_planes(nc.gpsimd, F32, w2_planes[:, 1, :], W2_scales[4:8], range(4))
 
         gains, shifts = [], []
         for two in range(2):

@@ -27,7 +27,7 @@ G1 = C // K_GROUP
 G2 = F // K_GROUP
 W1_HALF = F // 2
 W2_HALF = C // 2
-W2_PIECES = {1: (512, 512), 0: (512, 256, 128, 128)}
+W2_PIECES = {1: (512, 512), 0: (512, 256, 256)}
 LN_CHUNK = S // 4
 
 ROW_LN_W = 0
@@ -52,37 +52,40 @@ def tile_interactionblock_w_kernel(
             bank = psum.tile([P, BANK], F32, tag="bank", name="bank")
             return bank
 
-        ln_rows = keep.tile([P, BANK], BF16)
-        nc.vector.memset(ln_rows[:].bitcast(I32), 0)
-        bias_rows = keep.tile([P, BANK], BF16)
         w1_planes = keep.tile([P, F], U8, align_bytes=64)
         w2_planes = keep.tile([P, G2 // 4, C], U8, align_bytes=64)
+        ln_rows = keep.tile([P, BANK], BF16)
+        bias_rows = keep.tile([P, BANK], BF16)
+        nc.vector.memset(ln_rows[:].bitcast(I32), 0)
         nc.vector.memset(w1_planes[:].bitcast(I32), 0)
         nc.vector.memset(bias_rows[:].bitcast(I32), 0)
         nc.vector.memset(w2_planes[:].bitcast(I32), 0)
 
         ident_bf16 = keep.tile([P, P], BF16)
         make_identity(nc, ident_bf16[:])
-        ident_f32 = keep.tile([P, P], F32)
-        make_identity(nc, ident_f32[:])
-        minus_half = keep.tile([P, 4], F32)
-        nc.gpsimd.memset(minus_half[:], -0.5)
 
         def load_rows(tile, row, vector, width):
             rows = vector.rearrange("(r c) -> r c", c=width)
             nc.sync.dma_start(out=tile[row : row + rows.shape[0], 0:width], in_=rows)
 
-        def load_planes(engine, dtype, planes, scales, quads):
-            for quad in quads:
-                engine.dma_start(
-                    out=planes[32 * quad : 32 * quad + 16, :].bitcast(dtype),
-                    in_=scales[:, 4 * quad : 4 * quad + 4, :].bitcast(dtype),
+        def load_planes(planes, scales):
+            for quad in range(4):
+                nc.gpsimd.dma_start(
+                    out=planes[32 * quad : 32 * quad + 16, :].bitcast(F32),
+                    in_=scales[:, 4 * quad : 4 * quad + 4, :].bitcast(F32),
                 )
+
+        def hold_for_gpsimd(codes):
+            nc.gpsimd.memset(codes[:, 0:1], 0)
+
+        load_planes(w1_planes, W1_scales)
 
         w1 = {}
 
-        def load_w1(half, g):
+        def load_w1(half, g, hold=False):
             codes = keep.tile([P, W1_HALF], U32, name="w1_%d_%d" % (half, g), align_bytes=64)
+            if hold:
+                hold_for_gpsimd(codes)
             flat = W1_words[g].rearrange("p n t -> p (n t)")
             nc.sync.dma_start(
                 out=codes[:].bitcast(I32),
@@ -92,37 +95,23 @@ def tile_interactionblock_w_kernel(
 
         xs = keep.tile([P, S], BF16)
         nc.sync.dma_start(out=xs[:], in_=node_scalar)
+        load_rows(ln_rows, ROW_LN_W, ln_w, LN_CHUNK)
+        load_rows(ln_rows, ROW_LN_B, ln_b, LN_CHUNK)
         xe = keep.tile([P, ED], BF16)
         nc.sync.dma_start(out=xe[:], in_=node_equi)
-        load_rows(ln_rows, ROW_LN_W, ln_w, LN_CHUNK)
-        load_planes(nc.sync, I32, w1_planes, W1_scales, range(4))
         load_w1(0, 0)
-        load_rows(ln_rows, ROW_LN_B, ln_b, LN_CHUNK)
-        load_w1(0, 1)
         load_rows(bias_rows, ROW_B1, b1, BANK)
         load_rows(bias_rows, ROW_B2, b2, BANK)
-        for half, g in ((0, 2), (0, 3), (1, 0), (1, 1), (1, 2), (1, 3)):
-            load_w1(half, g)
+        load_w1(0, 1)
+        load_w1(0, 2)
+        load_w1(0, 3, hold=True)
+        load_w1(1, 0)
+        load_w1(1, 1)
 
-        load_planes(nc.gpsimd, F32, w2_planes[:, 0, :], W2_scales[0:4], range(0, 2))
-
-        w2_order = (1, 0)
-        w2 = {}
-        for half in w2_order:
-            for g in range(G2):
-                codes = keep.tile([P, W2_HALF], U32, name="w2_%d_%d" % (half, g), align_bytes=64)
-                flat = W2_words[g].rearrange("p n t -> p (n t)")
-                is_last = half == w2_order[-1] and g == G2 - 1
-                first = 0
-                for width in W2_PIECES[half] if is_last else (W2_HALF,):
-                    nc.sync.dma_start(
-                        out=codes[:, first : first + width].bitcast(I32),
-                        in_=flat[
-                            :, 4 * (W2_HALF * half + first) : 4 * (W2_HALF * half + first + width)
-                        ].bitcast(I32),
-                    )
-                    first += width
-                w2[(half, g)] = codes
+        ident_f32 = keep.tile([P, P], F32)
+        make_identity(nc, ident_f32[:])
+        minus_half = keep.tile([P, 4], F32)
+        nc.gpsimd.memset(minus_half[:], -0.5)
 
         def spread_two(vectors, row):
             bank = psum.tile([P, 2, BANK], BF16, tag="bank", name="spread")
@@ -185,8 +174,40 @@ def tile_interactionblock_w_kernel(
         nc.gpsimd.tensor_tensor(out=rnorms[:], in0=moments_eps[:], in1=minus_half[:], op=ALU.pow)
         ln_rstd = rnorms[:, 0:1]
 
-        load_planes(nc.gpsimd, F32, w2_planes[:, 0, :], W2_scales[0:4], range(2, 4))
-        load_planes(nc.gpsimd, F32, w2_planes[:, 1, :], W2_scales[4:8], range(4))
+        load_planes(w2_planes[:, 0, :], W2_scales[0:4])
+        load_w1(1, 2, hold=True)
+        load_w1(1, 3)
+
+        w2 = {}
+
+        def load_w2(half, groups, pieces, hold=False):
+            codes = keep.tile(
+                [P, len(groups), W2_HALF], U32, name="w2_%d_%d" % (half, groups[0]), align_bytes=64
+            )
+            if hold:
+                hold_for_gpsimd(codes[:, 0, :])
+            words = W2_words[groups[0] : groups[-1] + 1].rearrange("g p n t -> p g (n t)")
+            first = 0
+            for width in pieces:
+                column = W2_HALF * half + first
+                nc.sync.dma_start(
+                    out=codes[:, :, first : first + width].bitcast(I32),
+                    in_=words[:, :, 4 * column : 4 * (column + width)].bitcast(I32),
+                )
+                first += width
+            for i, g in enumerate(groups):
+                w2[(half, g)] = codes[:, i, :]
+
+        load_w2(1, (0, 1), (W2_HALF,))
+        load_planes(w2_planes[:, 1, :], W2_scales[4:8])
+        load_w2(1, (2, 3), (W2_HALF,), hold=True)
+        load_w2(1, (4, 5), (W2_HALF,))
+        load_w2(1, (6, 7), (W2_HALF,))
+        load_w2(0, (0, 1), (W2_HALF,))
+        load_w2(0, (2, 3), (W2_HALF,))
+        load_w2(0, (4, 5), (W2_HALF,))
+        load_w2(0, (6,), (W2_HALF,))
+        load_w2(0, (7,), W2_PIECES[0])
 
         gains, shifts = [], []
         for two in range(2):
@@ -345,19 +366,28 @@ def tile_interactionblock_w_kernel(
                     )
                     first += width
 
-        summed = keep.tile([P, C], F32)
+        result = keep.tile([P, S + ED], F32)
+        gates = keep.tile([P, C - S], F32)
 
         def finish(half, acc):
             first = half * W2_HALF
             for n, width in enumerate(W2_PIECES[half]):
+                last = min(first + width, S)
                 nc.vector.tensor_tensor(
-                    out=summed[:, first : first + width],
-                    in0=acc[n][:, 0:width],
-                    in1=addend[:, first : first + width],
+                    out=result[:, first:last],
+                    in0=acc[n][:, 0 : last - first],
+                    in1=addend[:, first:last],
                     op=ALU.add,
                 )
-                last = min(first + width, S)
-                nc.sync.dma_start(out=out[:, first:last], in_=summed[:, first:last])
+                if last < first + width:
+                    nc.vector.tensor_tensor(
+                        out=gates[:],
+                        in0=acc[n][:, last - first : width],
+                        in1=addend[:, last : first + width],
+                        op=ALU.add,
+                    )
+                if half == 0:
+                    nc.sync.dma_start(out=out[:, first:last], in_=result[:, first:last])
                 first += width
 
         acc_a = [new_bank() for n in range(W1_HALF // BANK)]
@@ -372,17 +402,17 @@ def tile_interactionblock_w_kernel(
         layer2(1, acc_upper, range(G2 // 2, G2))
         finish(1, acc_upper)
 
-        new_equi = keep.tile([P, ED], F32)
+        gated = keep.tile([P, ED], F32)
         for col, ch, channels, comps in BLOCKS:
             cols = slice(col, col + channels * comps)
             nc.vector.tensor_tensor(
-                out=new_equi[:, cols].rearrange("p (c d) -> p c d", d=comps),
+                out=gated[:, cols].rearrange("p (c d) -> p c d", d=comps),
                 in0=eb[:, cols].rearrange("p (c d) -> p c d", d=comps),
-                in1=summed[:, S + ch : S + ch + channels].unsqueeze(2).to_broadcast([P, channels, comps]),
+                in1=gates[:, ch : ch + channels].unsqueeze(2).to_broadcast([P, channels, comps]),
                 op=ALU.mult,
             )
-        nc.vector.tensor_tensor(out=new_equi[:], in0=new_equi[:], in1=xe[:], op=ALU.add)
-        nc.sync.dma_start(out=out[:, S : S + ED], in_=new_equi[:])
+        nc.vector.tensor_tensor(out=result[:, S : S + ED], in0=gated[:], in1=xe[:], op=ALU.add)
+        nc.sync.dma_start(out=out[:, W2_HALF : S + ED], in_=result[:, W2_HALF : S + ED])
 
         acc_lower = [new_bank() for width in W2_PIECES[0]]
         layer2(0, acc_lower, range(G2))

@@ -45,7 +45,7 @@ def tile_interactionblock_w_kernel(
     with ExitStack() as ctx:
         ctx.enter_context(tc.manual_schedule())
         keep = ctx.enter_context(tc.tile_pool(name="keep", bufs=1))
-        work = ctx.enter_context(tc.tile_pool(name="work", bufs=2))
+        work = ctx.enter_context(tc.tile_pool(name="work", bufs=4))
         psum = ctx.enter_context(tc.psum_pool(name="psum", bufs=8))
 
         def new_bank():
@@ -57,8 +57,8 @@ def tile_interactionblock_w_kernel(
         ln_rows = keep.tile([P, BANK], BF16)
         bias_rows = keep.tile([P, BANK], BF16)
         nc.vector.memset(ln_rows[:].bitcast(I32), 0)
-        nc.vector.memset(w1_planes[:].bitcast(I32), 0)
         nc.vector.memset(bias_rows[:].bitcast(I32), 0)
+        nc.vector.memset(w1_planes[:].bitcast(I32), 0)
         nc.vector.memset(w2_planes[:].bitcast(I32), 0)
 
         ident_bf16 = keep.tile([P, P], BF16)
@@ -68,8 +68,8 @@ def tile_interactionblock_w_kernel(
             rows = vector.rearrange("(r c) -> r c", c=width)
             nc.sync.dma_start(out=tile[row : row + rows.shape[0], 0:width], in_=rows)
 
-        def load_planes(planes, scales):
-            for quad in range(4):
+        def load_planes(planes, scales, quads):
+            for quad in quads:
                 nc.gpsimd.dma_start(
                     out=planes[32 * quad : 32 * quad + 16, :].bitcast(F32),
                     in_=scales[:, 4 * quad : 4 * quad + 4, :].bitcast(F32),
@@ -78,20 +78,23 @@ def tile_interactionblock_w_kernel(
         def hold_for_gpsimd(codes):
             nc.gpsimd.memset(codes[:, 0:1], 0)
 
-        load_planes(w1_planes, W1_scales)
-
-        w1 = {}
-
-        def load_w1(half, g, hold=False):
-            codes = keep.tile([P, W1_HALF], U32, name="w1_%d_%d" % (half, g), align_bytes=64)
-            if hold:
-                hold_for_gpsimd(codes)
-            flat = W1_words[g].rearrange("p n t -> p (n t)")
-            nc.sync.dma_start(
-                out=codes[:].bitcast(I32),
-                in_=flat[:, 4 * W1_HALF * half : 4 * W1_HALF * (half + 1)].bitcast(I32),
+        def load_codes(name, words, groups, first, width, pieces=None, hold=False):
+            codes = keep.tile(
+                [P, len(groups), width], U32, name="%s_%d_%d" % (name, groups[0], first), align_bytes=64
             )
-            w1[(half, g)] = codes
+            if hold:
+                hold_for_gpsimd(codes[:, 0, :])
+            flat = words[groups[0] : groups[-1] + 1].rearrange("g p n t -> p g (n t)")
+            done = 0
+            for piece in pieces or (width,):
+                nc.sync.dma_start(
+                    out=codes[:, :, done : done + piece].bitcast(I32),
+                    in_=flat[:, :, 4 * (first + done) : 4 * (first + done + piece)].bitcast(I32),
+                )
+                done += piece
+            return codes
+
+        load_planes(w1_planes, W1_scales, range(0, 2))
 
         xs = keep.tile([P, S], BF16)
         nc.sync.dma_start(out=xs[:], in_=node_scalar)
@@ -99,14 +102,13 @@ def tile_interactionblock_w_kernel(
         load_rows(ln_rows, ROW_LN_B, ln_b, LN_CHUNK)
         xe = keep.tile([P, ED], BF16)
         nc.sync.dma_start(out=xe[:], in_=node_equi)
-        load_w1(0, 0)
         load_rows(bias_rows, ROW_B1, b1, BANK)
         load_rows(bias_rows, ROW_B2, b2, BANK)
-        load_w1(0, 1)
-        load_w1(0, 2)
-        load_w1(0, 3, hold=True)
-        load_w1(1, 0)
-        load_w1(1, 1)
+        w1 = {}
+        codes = load_codes("w1", W1_words, (0, 1), 0, F)
+        for half in range(2):
+            for i in range(2):
+                w1[(half, i)] = codes[:, i, half * W1_HALF : (half + 1) * W1_HALF]
 
         ident_f32 = keep.tile([P, P], F32)
         make_identity(nc, ident_f32[:])
@@ -174,40 +176,29 @@ def tile_interactionblock_w_kernel(
         nc.gpsimd.tensor_tensor(out=rnorms[:], in0=moments_eps[:], in1=minus_half[:], op=ALU.pow)
         ln_rstd = rnorms[:, 0:1]
 
-        load_planes(w2_planes[:, 0, :], W2_scales[0:4])
-        load_w1(1, 2, hold=True)
-        load_w1(1, 3)
+        load_planes(w1_planes, W1_scales, range(2, 4))
+        codes = load_codes("w1", W1_words, (2,), 0, F, hold=True)
+        for half in range(2):
+            w1[(half, 2)] = codes[:, 0, half * W1_HALF : (half + 1) * W1_HALF]
+        for half in range(2):
+            codes = load_codes("w1", W1_words, (3,), half * W1_HALF, W1_HALF)
+            w1[(half, 3)] = codes[:, 0, :]
 
         w2 = {}
-
-        def load_w2(half, groups, pieces, hold=False):
-            codes = keep.tile(
-                [P, len(groups), W2_HALF], U32, name="w2_%d_%d" % (half, groups[0]), align_bytes=64
-            )
-            if hold:
-                hold_for_gpsimd(codes[:, 0, :])
-            words = W2_words[groups[0] : groups[-1] + 1].rearrange("g p n t -> p g (n t)")
-            first = 0
-            for width in pieces:
-                column = W2_HALF * half + first
-                nc.sync.dma_start(
-                    out=codes[:, :, first : first + width].bitcast(I32),
-                    in_=words[:, :, 4 * column : 4 * (column + width)].bitcast(I32),
-                )
-                first += width
-            for i, g in enumerate(groups):
-                w2[(half, g)] = codes[:, i, :]
-
-        load_w2(1, (0, 1), (W2_HALF,))
-        load_planes(w2_planes[:, 1, :], W2_scales[4:8])
-        load_w2(1, (2, 3), (W2_HALF,), hold=True)
-        load_w2(1, (4, 5), (W2_HALF,))
-        load_w2(1, (6, 7), (W2_HALF,))
-        load_w2(0, (0, 1), (W2_HALF,))
-        load_w2(0, (2, 3), (W2_HALF,))
-        load_w2(0, (4, 5), (W2_HALF,))
-        load_w2(0, (6,), (W2_HALF,))
-        load_w2(0, (7,), W2_PIECES[0])
+        load_planes(w2_planes[:, 0, :], W2_scales[0:4], range(4))
+        for first in (0, 2):
+            codes = load_codes("w2", W2_words, (first, first + 1), 0, C, hold=True)
+            for half in range(2):
+                for i in range(2):
+                    w2[(half, first + i)] = codes[:, i, half * W2_HALF : (half + 1) * W2_HALF]
+            if first == 0:
+                load_planes(w2_planes[:, 1, :], W2_scales[4:8], range(4))
+        for half, first in ((1, 4), (1, 6), (0, 4)):
+            codes = load_codes("w2", W2_words, (first, first + 1), half * W2_HALF, W2_HALF)
+            for i in range(2):
+                w2[(half, first + i)] = codes[:, i, :]
+        w2[(0, 6)] = load_codes("w2", W2_words, (6,), 0, W2_HALF)[:, 0, :]
+        w2[(0, 7)] = load_codes("w2", W2_words, (7,), 0, W2_HALF, W2_PIECES[0])[:, 0, :]
 
         gains, shifts = [], []
         for two in range(2):
@@ -328,32 +319,38 @@ def tile_interactionblock_w_kernel(
         h_codes = keep.tile([P, G2, P], U32, align_bytes=64)
         h_planes = keep.tile([P, G2, P], U8, align_bytes=64)
 
-        def silu_two_groups(pair, banks):
-            h = work.tile([P, 2 * K_GROUP], BF16)
-            for i in range(2):
-                first = (2 * pair + i) * BANK
-                biased = work.tile([P, BANK], F32)
-                nc.vector.tensor_tensor(
-                    out=biased[:], in0=banks[i][:], in1=b1_all[:, first : first + BANK], op=ALU.add
-                )
-                nc.scalar.activation(out=h[:, i * BANK : (i + 1) * BANK], in_=biased[:], func=ACT.Silu)
-            return h
+        h = keep.tile([P, F], BF16)
 
-        def activate(half, acc):
-            hs = [silu_two_groups(2 * half + j, acc[2 * j : 2 * j + 2]) for j in range(2)]
+        def silu(half, acc):
+            for n in range(W1_HALF // BANK):
+                cols = slice(half * W1_HALF + n * BANK, half * W1_HALF + (n + 1) * BANK)
+                biased = work.tile([P, BANK], F32)
+                nc.vector.tensor_tensor(out=biased[:], in0=acc[n][:], in1=b1_all[:, cols], op=ALU.add)
+                nc.scalar.activation(out=h[:, cols], in_=biased[:], func=ACT.Silu)
+
+        def transpose_h(half):
+            first = half * W1_HALF
+            return [
+                transpose_two_groups(h[:, first + 2 * K_GROUP * j : first + 2 * K_GROUP * (j + 1)])
+                for j in range(2)
+            ]
+
+        def quantise_h(half, grouped):
             for j in range(2):
                 groups = slice(4 * half + 2 * j, 4 * half + 2 * j + 2)
-                grouped = transpose_two_groups(hs[j][:])
                 nc.vector.quantize_mx(
                     out=h_codes[:, groups, :].rearrange("p g m -> p (g m)").bitcast(FP8X4),
                     scales=h_planes[:, groups, :].rearrange("p g m -> p (g m)"),
-                    in_=grouped[:],
+                    in_=grouped[j][:],
                 )
 
-        def layer2(half, acc, groups):
+        def layer2(half, acc, groups, banks=None):
             for g in groups:
                 first = 0
                 for n, width in enumerate(W2_PIECES[half]):
+                    if banks and n not in banks:
+                        first += width
+                        continue
                     cols = slice(half * W2_HALF + first, half * W2_HALF + first + width)
                     nc.tensor.matmul_mx(
                         out=acc[n][:, 0:width],
@@ -369,39 +366,31 @@ def tile_interactionblock_w_kernel(
         result = keep.tile([P, S + ED], F32)
         gates = keep.tile([P, C - S], F32)
 
-        def finish(half, acc):
-            first = half * W2_HALF
-            for n, width in enumerate(W2_PIECES[half]):
-                last = min(first + width, S)
-                nc.vector.tensor_tensor(
-                    out=result[:, first:last],
-                    in0=acc[n][:, 0 : last - first],
-                    in1=addend[:, first:last],
-                    op=ALU.add,
-                )
-                if last < first + width:
-                    nc.vector.tensor_tensor(
-                        out=gates[:],
-                        in0=acc[n][:, last - first : width],
-                        in1=addend[:, last : first + width],
-                        op=ALU.add,
-                    )
-                if half == 0:
-                    nc.sync.dma_start(out=out[:, first:last], in_=result[:, first:last])
-                first += width
+        def add_piece(acc, first, last, target):
+            nc.vector.tensor_tensor(out=target, in0=acc, in1=addend[:, first:last], op=ALU.add)
 
         acc_a = [new_bank() for n in range(W1_HALF // BANK)]
-        layer1(0, acc_a, range(G1))
         acc_b = [new_bank() for n in range(W1_HALF // BANK)]
-        layer1(1, acc_b, range(G1 - 1))
-        activate(0, acc_a)
-        layer1(1, acc_b, range(G1 - 1, G1))
+        for groups in ((0, 1), (2,), (3,)):
+            layer1(0, acc_a, groups)
+            layer1(1, acc_b, groups)
+        silu(0, acc_a)
+        grouped_a = transpose_h(0)
+        silu(1, acc_b)
+        quantise_h(0, grouped_a)
         acc_upper = [new_bank() for width in W2_PIECES[1]]
-        layer2(1, acc_upper, range(G2 // 2))
-        activate(1, acc_b)
-        layer2(1, acc_upper, range(G2 // 2, G2))
-        finish(1, acc_upper)
-
+        acc_lower = [new_bank() for width in W2_PIECES[0]]
+        layer2(1, acc_upper, (0, 1))
+        layer2(0, acc_lower, (0, 1))
+        grouped_b = transpose_h(1)
+        quantise_h(1, grouped_b)
+        layer2(1, acc_upper, (2, 3))
+        layer2(0, acc_lower, (2, 3))
+        layer2(1, acc_upper, (4, 5))
+        layer2(1, acc_upper, (6, 7), banks=(1,))
+        layer2(1, acc_upper, (6, 7), banks=(0,))
+        first = C - BANK
+        add_piece(acc_upper[1][:, S - first : BANK], S, C, gates[:])
         gated = keep.tile([P, ED], F32)
         for col, ch, channels, comps in BLOCKS:
             cols = slice(col, col + channels * comps)
@@ -412,8 +401,14 @@ def tile_interactionblock_w_kernel(
                 op=ALU.mult,
             )
         nc.vector.tensor_tensor(out=result[:, S : S + ED], in0=gated[:], in1=xe[:], op=ALU.add)
+        add_piece(acc_upper[1][:, 0 : S - first], first, S, result[:, first:S])
+        add_piece(acc_upper[0][:], W2_HALF, first, result[:, W2_HALF:first])
         nc.sync.dma_start(out=out[:, W2_HALF : S + ED], in_=result[:, W2_HALF : S + ED])
 
-        acc_lower = [new_bank() for width in W2_PIECES[0]]
-        layer2(0, acc_lower, range(G2))
-        finish(0, acc_lower)
+        layer2(0, acc_lower, range(G2 // 2, G2))
+        first = 0
+        for acc, width in zip(acc_lower, W2_PIECES[0]):
+            cols = slice(first, first + width)
+            add_piece(acc[:, 0:width], first, first + width, result[:, cols])
+            nc.sync.dma_start(out=out[:, cols], in_=result[:, cols])
+            first += width

@@ -52,8 +52,8 @@ def tile_interactionblock_w_kernel(
             bank = psum.tile([P, BANK], F32, tag="bank", name="bank")
             return bank
 
-        w1_planes = keep.tile([P, F], U8, align_bytes=64)
-        w2_planes = keep.tile([P, G2 // 4, C], U8, align_bytes=64)
+        w1_planes = keep.tile([P, F], U8, align_bytes=256)
+        w2_planes = keep.tile([P, G2 // 4, C], U8, align_bytes=256)
         ln_rows = keep.tile([P, BANK], BF16)
         bias_rows = keep.tile([P, BANK], BF16)
         nc.vector.memset(ln_rows[:].bitcast(I32), 0)
@@ -80,7 +80,7 @@ def tile_interactionblock_w_kernel(
 
         def load_codes(name, words, groups, first, width, pieces=None, hold=False):
             codes = keep.tile(
-                [P, len(groups), width], U32, name="%s_%d_%d" % (name, groups[0], first), align_bytes=64
+                [P, len(groups), width], U32, name="%s_%d_%d" % (name, groups[0], first), align_bytes=256
             )
             if hold:
                 hold_for_gpsimd(codes[:, 0, :])
@@ -96,11 +96,11 @@ def tile_interactionblock_w_kernel(
 
         load_planes(w1_planes, W1_scales, range(0, 2))
 
-        xs = keep.tile([P, S], BF16)
+        xs = keep.tile([P, S], BF16, align_bytes=256)
         nc.sync.dma_start(out=xs[:], in_=node_scalar)
         load_rows(ln_rows, ROW_LN_W, ln_w, LN_CHUNK)
         load_rows(ln_rows, ROW_LN_B, ln_b, LN_CHUNK)
-        xe = keep.tile([P, ED], BF16)
+        xe = keep.tile([P, ED], BF16, align_bytes=256)
         nc.sync.dma_start(out=xe[:], in_=node_equi)
         load_rows(bias_rows, ROW_B1, b1, BANK)
         load_rows(bias_rows, ROW_B2, b2, BANK)
@@ -363,7 +363,7 @@ def tile_interactionblock_w_kernel(
                     )
                     first += width
 
-        result = keep.tile([P, S + ED], F32)
+        result = keep.tile([P, S + ED], F32, align_bytes=256)
         gates = keep.tile([P, C - S], F32)
 
         def add_piece(acc, first, last, target):

from contextlib import ExitStack

import concourse.mybir as mybir
from concourse.masks import make_identity

F32 = mybir.dt.float32
BF16 = mybir.dt.bfloat16
I32 = mybir.dt.int32
U32 = mybir.dt.uint32
U8 = mybir.dt.uint8
FP8X4 = mybir.dt.float8_e4m3fn_x4
ALU = mybir.AluOpType
ACT = mybir.ActivationFunctionType
AXIS = mybir.AxisListType

P = 128
S = 1824
ED = 480
C = 2048
F = 4096
EPS = 1e-5
BLOCKS = ((0, 0, 128, 1), (128, 128, 64, 3), (320, 192, 32, 5))

K_GROUP = 512
BANK = 512
G1 = C // K_GROUP
G2 = F // K_GROUP
W1_HALF = F // 2
W2_HALF = C // 2
W2_PIECES = {1: (512, 512), 0: (512, 256, 256)}
LN_CHUNK = S // 4

ROW_LN_W = 0
ROW_LN_B = 4
ROW_B1 = 0
ROW_B2 = 8

FLOPS = 2 * P * C * F * 2


def tile_interactionblock_w_kernel(
    tc, node_scalar, node_equi, ln_w, ln_b, W1_words, W1_scales, b1, W2_words, W2_scales, b2, out
):
    nc = tc.nc
    with ExitStack() as ctx:
        ctx.enter_context(tc.manual_schedule())
        keep = ctx.enter_context(tc.tile_pool(name="keep", bufs=1))
        work = ctx.enter_context(tc.tile_pool(name="work", bufs=4))
        psum = ctx.enter_context(tc.psum_pool(name="psum", bufs=8))

        def new_bank():
            bank = psum.tile([P, BANK], F32, tag="bank", name="bank")
            return bank

        w1_planes = keep.tile([P, F], U8, align_bytes=256)
        w2_planes = keep.tile([P, G2 // 4, C], U8, align_bytes=256)
        ln_rows = keep.tile([P, BANK], BF16)
        bias_rows = keep.tile([P, BANK], BF16)
        nc.vector.memset(ln_rows[:].bitcast(I32), 0)
        nc.vector.memset(bias_rows[:].bitcast(I32), 0)
        nc.vector.memset(w1_planes[:].bitcast(I32), 0)
        nc.vector.memset(w2_planes[:].bitcast(I32), 0)

        ident_bf16 = keep.tile([P, P], BF16)
        make_identity(nc, ident_bf16[:])

        def load_rows(tile, row, vector, width):
            rows = vector.rearrange("(r c) -> r c", c=width)
            nc.sync.dma_start(out=tile[row : row + rows.shape[0], 0:width], in_=rows)

        def load_planes(planes, scales, quads):
            for quad in quads:
                nc.gpsimd.dma_start(
                    out=planes[32 * quad : 32 * quad + 16, :].bitcast(F32),
                    in_=scales[:, 4 * quad : 4 * quad + 4, :].bitcast(F32),
                )

        def hold_for_gpsimd(codes):
            nc.gpsimd.memset(codes[:, 0:1], 0)

        def load_codes(name, words, groups, first, width, pieces=None, hold=False):
            codes = keep.tile(
                [P, len(groups), width], U32, name="%s_%d_%d" % (name, groups[0], first), align_bytes=256
            )
            if hold:
                hold_for_gpsimd(codes[:, 0, :])
            flat = words[groups[0] : groups[-1] + 1].rearrange("g p n t -> p g (n t)")
            done = 0
            for piece in pieces or (width,):
                nc.sync.dma_start(
                    out=codes[:, :, done : done + piece].bitcast(I32),
                    in_=flat[:, :, 4 * (first + done) : 4 * (first + done + piece)].bitcast(I32),
                )
                done += piece
            return codes

        load_planes(w1_planes, W1_scales, range(0, 2))

        xs = keep.tile([P, S], BF16, align_bytes=256)
        nc.sync.dma_start(out=xs[:], in_=node_scalar)
        load_rows(ln_rows, ROW_LN_W, ln_w, LN_CHUNK)
        load_rows(ln_rows, ROW_LN_B, ln_b, LN_CHUNK)
        xe = keep.tile([P, ED], BF16, align_bytes=256)
        nc.sync.dma_start(out=xe[:], in_=node_equi)
        load_rows(bias_rows, ROW_B1, b1, BANK)
        load_rows(bias_rows, ROW_B2, b2, BANK)
        w1 = {}
        codes = load_codes("w1", W1_words, (0, 1), 0, F)
        for half in range(2):
            for i in range(2):
                w1[(half, i)] = codes[:, i, half * W1_HALF : (half + 1) * W1_HALF]

        ident_f32 = keep.tile([P, P], F32)
        make_identity(nc, ident_f32[:])
        minus_half = keep.tile([P, 4], F32)
        nc.gpsimd.memset(minus_half[:], -0.5)

        def spread_two(vectors, row):
            bank = psum.tile([P, 2, BANK], BF16, tag="bank", name="spread")
            for i in range(2):
                nc.tensor.matmul(
                    out=bank[:, i, :],
                    lhsT=ident_bf16[:, row + i : row + i + 1].to_broadcast([P, P]),
                    rhs=vectors[:],
                    start=True,
                    stop=True,
                )
            return bank

        def transpose_two_groups(values):
            words = values.bitcast(F32)
            bank = new_bank()
            for i in range(2):
                for u in range(2):
                    nc.tensor.transpose(
                        bank[:, (2 * i + u) * P : (2 * i + u + 1) * P],
                        words[:, 256 * i + u : 256 * (i + 1) : 2],
                        ident_f32[:],
                    )
            grouped = work.tile([P, 2 * K_GROUP], BF16, align_bytes=64)
            nc.scalar.copy(
                out=grouped[:].bitcast(F32).rearrange("p (i m u) -> p i m u", i=2, u=2),
                in_=bank[:].rearrange("p (i u m) -> p i m u", i=2, u=2),
            )
            return grouped

        scratch = keep.tile([P, ED], F32)
        minus_mean0 = keep.tile([P, 1], F32)
        nc.scalar.activation(
            out=scratch[:, 0:P], in_=xe[:, 0:P], func=ACT.Copy, scale=-1.0 / P, accum_out=minus_mean0[:]
        )
        centred0 = keep.tile([P, P], F32)
        nc.scalar.activation(out=centred0[:], in_=xe[:, 0:P], func=ACT.Identity, bias=minus_mean0[:])
        block_in = [centred0[:]] + [
            xe[:, col : col + channels * comps] for col, ch, channels, comps in BLOCKS[1:]
        ]
        moments = keep.tile([P, 5], F32)
        for l, (col, ch, channels, comps) in enumerate(BLOCKS):
            nc.scalar.activation(
                out=scratch[:, col : col + channels * comps],
                in_=block_in[l],
                func=ACT.Square,
                scale=channels**-0.5,
                accum_out=moments[:, 2 + l : 3 + l],
            )

        ln_stats = keep.tile([P, 4, 6], F32)
        for c in range(4):
            nc.vector.bn_stats(out=ln_stats[:, c, :], in_=xs[:, c * LN_CHUNK : (c + 1) * LN_CHUNK])
        nc.vector.bn_aggr(out=moments[:, 0:2], in_=ln_stats[:].rearrange("p c s -> p (c s)"))
        ln_mean = moments[:, 0:1]

        moments_eps = keep.tile([P, 4], F32)
        nc.gpsimd.tensor_scalar_add(moments_eps[:], moments[:, 1:5], EPS)
        rnorms = keep.tile([P, 4], F32)
        nc.gpsimd.tensor_tensor(out=rnorms[:], in0=moments_eps[:], in1=minus_half[:], op=ALU.pow)
        ln_rstd = rnorms[:, 0:1]

        load_planes(w1_planes, W1_scales, range(2, 4))
        codes = load_codes("w1", W1_words, (2,), 0, F, hold=True)
        for half in range(2):
            w1[(half, 2)] = codes[:, 0, half * W1_HALF : (half + 1) * W1_HALF]
        for half in range(2):
            codes = load_codes("w1", W1_words, (3,), half * W1_HALF, W1_HALF)
            w1[(half, 3)] = codes[:, 0, :]

        w2 = {}
        load_planes(w2_planes[:, 0, :], W2_scales[0:4], range(4))
        for first in (0, 2):
            codes = load_codes("w2", W2_words, (first, first + 1), 0, C, hold=True)
            for half in range(2):
                for i in range(2):
                    w2[(half, first + i)] = codes[:, i, half * W2_HALF : (half + 1) * W2_HALF]
            if first == 0:
                load_planes(w2_planes[:, 1, :], W2_scales[4:8], range(4))
        for half, first in ((1, 4), (1, 6), (0, 4)):
            codes = load_codes("w2", W2_words, (first, first + 1), half * W2_HALF, W2_HALF)
            for i in range(2):
                w2[(half, first + i)] = codes[:, i, :]
        w2[(0, 6)] = load_codes("w2", W2_words, (6,), 0, W2_HALF)[:, 0, :]
        w2[(0, 7)] = load_codes("w2", W2_words, (7,), 0, W2_HALF, W2_PIECES[0])[:, 0, :]

        gains, shifts = [], []
        for two in range(2):
            gains.append(spread_two(ln_rows, ROW_LN_W + 2 * two))
            shifts.append(spread_two(ln_rows, ROW_LN_B + 2 * two))
        b1_banks = [spread_two(bias_rows, ROW_B1 + 2 * two) for two in range(F // (2 * BANK))]

        eb = keep.tile([P, ED], F32)
        inv = keep.tile([P, C - S], F32)
        for l, (col, ch, channels, comps) in enumerate(BLOCKS):
            cols = slice(col, col + channels * comps)
            nc.scalar.activation(
                out=eb[:, cols], in_=block_in[l], func=ACT.Copy, scale=rnorms[:, 1 + l : 2 + l]
            )
            nc.scalar.activation(
                out=scratch[:, cols], in_=eb[:, cols], func=ACT.Square, scale=comps**-0.25
            )

        b1_all = keep.tile([P, F], BF16)

        def keep_b1(two):
            nc.scalar.copy(
                out=b1_all[:, 2 * BANK * two : 2 * BANK * (two + 1)],
                in_=b1_banks[two][:].rearrange("p i n -> p (i n)"),
            )

        cat = keep.tile([P, C], BF16)

        def norm_quarter(c):
            first = c * LN_CHUNK
            scaled = work.tile([P, LN_CHUNK], F32)
            nc.vector.scalar_tensor_tensor(
                out=scaled[:],
                in0=xs[:, first : first + LN_CHUNK],
                scalar=ln_mean,
                in1=gains[c // 2][:, c % 2, 0:LN_CHUNK],
                op0=ALU.subtract,
                op1=ALU.mult,
            )
            nc.vector.scalar_tensor_tensor(
                out=cat[:, first : first + LN_CHUNK],
                in0=scaled[:],
                scalar=ln_rstd,
                in1=shifts[c // 2][:, c % 2, 0:LN_CHUNK],
                op0=ALU.mult,
                op1=ALU.add,
            )

        cat_codes = keep.tile([P, G1, P], U32, align_bytes=64)
        cat_planes = keep.tile([P, G1, P], U8, align_bytes=64)

        def transpose_cat(pair):
            return transpose_two_groups(cat[:, 2 * K_GROUP * pair : 2 * K_GROUP * (pair + 1)])

        def quantise_cat(pair, grouped):
            groups = slice(2 * pair, 2 * pair + 2)
            nc.vector.quantize_mx(
                out=cat_codes[:, groups, :].rearrange("p g m -> p (g m)").bitcast(FP8X4),
                scales=cat_planes[:, groups, :].rearrange("p g m -> p (g m)"),
                in_=grouped[:],
            )

        norm_quarter(0)
        norm_quarter(1)
        norm_quarter(2)
        keep_b1(0)
        keep_b1(1)
        grouped0 = transpose_cat(0)
        for col, ch, channels, comps in BLOCKS:
            nc.vector.tensor_reduce(
                out=inv[:, ch : ch + channels],
                in_=scratch[:, col : col + channels * comps].rearrange("p (c d) -> p c d", d=comps),
                axis=AXIS.X,
                op=ALU.add,
            )
        nc.vector.tensor_copy(out=cat[:, S:C], in_=inv[:])
        norm_quarter(3)
        quantise_cat(0, grouped0)
        grouped1 = transpose_cat(1)
        keep_b1(2)
        keep_b1(3)
        b2_banks = [spread_two(bias_rows, ROW_B2 + 2 * two) for two in range(C // (2 * BANK))]

        quantise_cat(1, grouped1)

        addend = keep.tile([P, C], F32)
        for two in range(C // (2 * BANK)):
            bank = b2_banks[two]
            for i in range(2):
                first = (2 * two + i) * BANK
                width = min(BANK, S - first)
                nc.vector.tensor_tensor(
                    out=addend[:, first : first + width],
                    in0=bank[:, i, 0:width],
                    in1=xs[:, first : first + width],
                    op=ALU.add,
                )
                if width < BANK:
                    nc.vector.tensor_copy(
                        out=addend[:, first + width : first + BANK], in_=bank[:, i, width:BANK]
                    )

        def layer1(half, acc, groups):
            for g in groups:
                for n in range(W1_HALF // BANK):
                    nc.tensor.matmul_mx(
                        out=acc[n][:],
                        lhsT=cat_codes[:, g, :].bitcast(FP8X4),
                        lhsT_scale=cat_planes[:, g, :],
                        rhs=w1[(half, g)][:, n * BANK : (n + 1) * BANK].bitcast(FP8X4),
                        rhs_scale=w1_planes[
                            4 * g : P, half * W1_HALF + n * BANK : half * W1_HALF + (n + 1) * BANK
                        ],
                        start=(g == 0),
                        stop=(g == G1 - 1),
                    )

        h_codes = keep.tile([P, G2, P], U32, align_bytes=64)
        h_planes = keep.tile([P, G2, P], U8, align_bytes=64)

        h = keep.tile([P, F], BF16)

        def silu(half, acc):
            for n in range(W1_HALF // BANK):
                cols = slice(half * W1_HALF + n * BANK, half * W1_HALF + (n + 1) * BANK)
                biased = work.tile([P, BANK], F32)
                nc.vector.tensor_tensor(out=biased[:], in0=acc[n][:], in1=b1_all[:, cols], op=ALU.add)
                nc.scalar.activation(out=h[:, cols], in_=biased[:], func=ACT.Silu)

        def transpose_h(half):
            first = half * W1_HALF
            return [
                transpose_two_groups(h[:, first + 2 * K_GROUP * j : first + 2 * K_GROUP * (j + 1)])
                for j in range(2)
            ]

        def quantise_h(half, grouped):
            for j in range(2):
                groups = slice(4 * half + 2 * j, 4 * half + 2 * j + 2)
                nc.vector.quantize_mx(
                    out=h_codes[:, groups, :].rearrange("p g m -> p (g m)").bitcast(FP8X4),
                    scales=h_planes[:, groups, :].rearrange("p g m -> p (g m)"),
                    in_=grouped[j][:],
                )

        def layer2(half, acc, groups, banks=None):
            for g in groups:
                first = 0
                for n, width in enumerate(W2_PIECES[half]):
                    if banks and n not in banks:
                        first += width
                        continue
                    cols = slice(half * W2_HALF + first, half * W2_HALF + first + width)
                    nc.tensor.matmul_mx(
                        out=acc[n][:, 0:width],
                        lhsT=h_codes[:, g, :].bitcast(FP8X4),
                        lhsT_scale=h_planes[:, g, :],
                        rhs=w2[(half, g)][:, first : first + width].bitcast(FP8X4),
                        rhs_scale=w2_planes[4 * (g % 4) : P, g // 4, cols],
                        start=(g == 0),
                        stop=(g == G2 - 1),
                    )
                    first += width

        result = keep.tile([P, S + ED], F32, align_bytes=256)
        gates = keep.tile([P, C - S], F32)

        def add_piece(acc, first, last, target):
            nc.vector.tensor_tensor(out=target, in0=acc, in1=addend[:, first:last], op=ALU.add)

        acc_a = [new_bank() for n in range(W1_HALF // BANK)]
        acc_b = [new_bank() for n in range(W1_HALF // BANK)]
        for groups in ((0, 1), (2,), (3,)):
            layer1(0, acc_a, groups)
            layer1(1, acc_b, groups)
        silu(0, acc_a)
        grouped_a = transpose_h(0)
        silu(1, acc_b)
        quantise_h(0, grouped_a)
        acc_upper = [new_bank() for width in W2_PIECES[1]]
        acc_lower = [new_bank() for width in W2_PIECES[0]]
        layer2(1, acc_upper, (0, 1))
        layer2(0, acc_lower, (0, 1))
        grouped_b = transpose_h(1)
        quantise_h(1, grouped_b)
        layer2(1, acc_upper, (2, 3))
        layer2(0, acc_lower, (2, 3))
        layer2(1, acc_upper, (4, 5))
        layer2(1, acc_upper, (6, 7), banks=(1,))
        layer2(1, acc_upper, (6, 7), banks=(0,))
        first = C - BANK
        add_piece(acc_upper[1][:, S - first : BANK], S, C, gates[:])
        gated = keep.tile([P, ED], F32)
        for col, ch, channels, comps in BLOCKS:
            cols = slice(col, col + channels * comps)
            nc.vector.tensor_tensor(
                out=gated[:, cols].rearrange("p (c d) -> p c d", d=comps),
                in0=eb[:, cols].rearrange("p (c d) -> p c d", d=comps),
                in1=gates[:, ch : ch + channels].unsqueeze(2).to_broadcast([P, channels, comps]),
                op=ALU.mult,
            )
        nc.vector.tensor_tensor(out=result[:, S : S + ED], in0=gated[:], in1=xe[:], op=ALU.add)
        add_piece(acc_upper[1][:, 0 : S - first], first, S, result[:, first:S])
        add_piece(acc_upper[0][:], W2_HALF, first, result[:, W2_HALF:first])
        nc.sync.dma_start(out=out[:, W2_HALF : S + ED], in_=result[:, W2_HALF : S + ED])

        layer2(0, acc_lower, range(G2 // 2, G2))
        first = 0
        for acc, width in zip(acc_lower, W2_PIECES[0]):
            cols = slice(first, first + width)
            add_piece(acc[:, 0:width], first, first + width, result[:, cols])
            nc.sync.dma_start(out=out[:, cols], in_=result[:, cols])
            first += width
